import numpy as np
import ml_dtypes


def mxq(x, axis, fmt="e4m3"):
    dtype, down = {"e4m3": (ml_dtypes.float8_e4m3fn, 7), "e5m2": (ml_dtypes.float8_e5m2, 14)}[fmt]
    v = np.moveaxis(np.asarray(x, np.float32).astype(ml_dtypes.bfloat16).astype(np.float64), axis, -1)
    blocks = v.reshape(v.shape[:-1] + (-1, 32))
    amax = np.abs(blocks).max(-1, keepdims=True)
    byte = np.maximum(np.where(amax > 0, np.frexp(amax)[1] - 1 + 127, 0) - down, 1)
    scale = np.exp2(byte - 127.0)
    codes = (blocks / scale).astype(np.float32).astype(dtype).astype(np.float64)
    return np.moveaxis((codes * scale).reshape(v.shape), -1, axis)


WIDE = False


def mx_kscale(k):
    if not WIDE:
        return np.ones(k)
    levels = np.array([10, -10, 5, -5, 0])
    a = np.random.permutation(np.resize(levels, k // 512 * 4)).reshape(k // 512, 4)
    idx = np.arange(k)
    return np.exp2(a[idx // 512, idx % 128 // 32])


BF16 = ml_dtypes.bfloat16


def bf(x):
    return np.asarray(x, np.float32).astype(BF16)


def f64(x):
    return np.asarray(x).astype(np.float64)


B, C, H, W, RQ, RV = 1, 512, 64, 64, 4, 1
DQ, DV = C // RQ, C // RV
N = H * W
M = (H // 2) * (W // 2)


def setup_inputs():
    t = mx_kscale(DV)
    return {"q": bf(np.random.standard_normal((B, DQ, N)) * 8.0 / np.sqrt(DQ)),
            "k_pool": bf(0.5 + 0.35 * np.random.standard_normal((B, DQ, M))),
            "v_pool": bf((0.5 + 0.35 * np.random.standard_normal((B, DV, M))) * t[None, :, None]),
            "imgs": bf(np.random.standard_normal((B, C, H, W))),
            "w_out": bf(np.random.standard_normal((C, DV)) * 1.5 / np.sqrt(DV) / t[None, :]),
            "gain": bf(1.0 + 0.1 * np.random.standard_normal(1))}


def reference(q, k_pool, v_pool, imgs, w_out, gain):
    s = f64(q).transpose(0, 2, 1) @ f64(k_pool)
    e = np.exp(s - s.max(-1, keepdims=True))
    att = (mxq(e, 2, "e4m3") @ mxq(f64(v_pool), 2, "e4m3").transpose(0, 2, 1)) / e.sum(-1, keepdims=True)
    y = mxq(att, 2, "e4m3") @ mxq(f64(w_out), 1, "e4m3").T
    return f64(imgs) + y.transpose(0, 2, 1).reshape(B, C, H, W) * f64(gain)

@@ -1,0 +1,253 @@
+from contextlib import ExitStack
+
+import concourse.mybir as mybir
+from concourse.masks import make_identity
+
+F32 = mybir.dt.float32
+BF16 = mybir.dt.bfloat16
+U32 = mybir.dt.uint32
+U8 = mybir.dt.uint8
+FP8X4 = mybir.dt.float8_e4m3fn_x4
+ACT = mybir.ActivationFunctionType
+ALU = mybir.AluOpType
+AX = mybir.AxisListType
+
+P = 128
+PACK = 4
+BANK = 512
+N_PIX = 4096
+M_POS = 1024
+DV = 512
+C_OUT = 512
+M_PASSES = M_POS // (P * PACK)
+M_HALVES = M_POS // BANK
+TILES = N_PIX // P
+GROUP = 4
+GROUPS = TILES // GROUP
+CHUNKS = 4
+
+FLOPS = 2 * N_PIX * M_POS * P + 2 * N_PIX * M_POS * DV + 2 * N_PIX * DV * C_OUT
+
+
+def tile_selfattentionconv2d_pb_t_kernel(tc, q, k_pool, v_pool, imgs, w_out, gain, out):
+    nc = tc.nc
+    with ExitStack() as ctx:
+        keep = ctx.enter_context(tc.tile_pool(name="keep", bufs=1))
+        small = ctx.enter_context(tc.tile_pool(name="small", bufs=4))
+        work = ctx.enter_context(tc.tile_pool(name="work", bufs=3))
+        codes = ctx.enter_context(tc.tile_pool(name="codes", bufs=7))
+        pair = ctx.enter_context(tc.tile_pool(name="pair", bufs=2))
+        stores = ctx.enter_context(tc.tile_pool(name="stores", bufs=4))
+        psum_s = ctx.enter_context(tc.psum_pool(name="psum_s", bufs=4))
+        psum_t = ctx.enter_context(tc.psum_pool(name="psum_t", bufs=2))
+        psum_o = ctx.enter_context(tc.psum_pool(name="psum_o", bufs=2))
+
+        q_sb = keep.tile([P, N_PIX], BF16)
+        k_sb = keep.tile([P, M_POS], BF16)
+        v_sb = keep.tile([P, CHUNKS, M_POS], BF16)
+        w_sb = keep.tile([P, CHUNKS, DV], BF16)
+        imgs_sb = keep.tile([P, CHUNKS, N_PIX], BF16)
+        gain_bf = keep.tile([P, 1], BF16)
+        q_view = q.rearrange("b d n -> (b d) n")
+        imgs_view = imgs.rearrange("b (c p) h w -> p (b c) (h w)", p=P)
+        out_view = out.rearrange("b (c p) h w -> p (b c) (h w)", p=P)
+        quarter = N_PIX // 4
+        nc.sync.dma_start(out=k_sb[:], in_=k_pool.rearrange("b d m -> (b d) m"))
+        nc.sync.dma_start(out=q_sb[:, 0:quarter], in_=q_view[:, 0:quarter])
+        nc.sync.dma_start(out=v_sb[:], in_=v_pool.rearrange("b (c p) m -> p (b c) m", p=P))
+        for piece in range(1, 4):
+            cols = slice(piece * quarter, (piece + 1) * quarter)
+            nc.sync.dma_start(out=q_sb[:, cols], in_=q_view[:, cols])
+        nc.sync.dma_start(out=w_sb[:], in_=w_out.rearrange("(c p) d -> p c d", p=P))
+        nc.scalar.dma_start(out=gain_bf[:], in_=gain.partition_broadcast(P))
+        for c in range(CHUNKS):
+            nc.sync.dma_start(out=imgs_sb[:, c, :], in_=imgs_view[:, c, :])
+
+        ident_bf = keep.tile([P, P], BF16)
+        make_identity(nc, ident_bf[:])
+        ident_f32 = keep.tile([P, P], F32)
+        make_identity(nc, ident_f32[:])
+        gain_f32 = keep.tile([P, 1], F32)
+        nc.vector.tensor_copy(out=gain_f32[:], in_=gain_bf[:])
+
+        def transpose_and_group(blocks, grouped):
+            turned = psum_t.tile([P, 2 * PACK, P], BF16, tag="turned")
+            for index, block in enumerate(blocks):
+                nc.tensor.transpose(turned[:, index, :], block, ident_bf[:])
+            nc.scalar.copy(out=grouped, in_=turned[:].rearrange("p (r t) n -> p r n t", t=PACK))
+
+        def quantise_weights(rows_sb, passes, name):
+            grouped = keep.tile([P, passes, CHUNKS * P, PACK], BF16, align_bytes=64, name=name + "_grouped")
+            words = keep.tile([P, passes, CHUNKS * P], U32, align_bytes=64, name=name + "_words")
+            scales = keep.tile([P, passes, CHUNKS * P], U8, align_bytes=64, name=name + "_scales")
+            for g in range(passes):
+                for half in range(CHUNKS // 2):
+                    blocks = [
+                        rows_sb[:, 2 * half + r, (PACK * g + t) * P : (PACK * g + t + 1) * P]
+                        for r in range(2)
+                        for t in range(PACK)
+                    ]
+                    rows = slice(2 * half * P, (2 * half + 2) * P)
+                    transpose_and_group(blocks, grouped[:, g, rows, :].rearrange("p (r n) t -> p r n t", r=2))
+            for g in range(passes):
+                nc.vector.quantize_mx(
+                    out=words[:, g, :].bitcast(FP8X4),
+                    scales=scales[:, g, :],
+                    in_=grouped[:, g, :, :].rearrange("p n t -> p (n t)"),
+                )
+            return words, scales
+
+        v_words, v_scales = quantise_weights(v_sb, M_PASSES, "v")
+        w_words, w_scales = quantise_weights(w_sb, 1, "w")
+
+        e_rows = {}
+        e_grouped = {}
+        e_packed = {}
+        row_sums = {}
+        inverse_sums = {}
+        att_grouped = {}
+
+        def scores_and_exp(i):
+            group, j = divmod(i, GROUP)
+            if j == 0:
+                row_sums[group] = pair.tile([P, GROUP, M_HALVES], F32, name="row_sums")
+            s_ps = [psum_s.tile([P, BANK], F32, name="s_ps") for h in range(M_HALVES)]
+            half_max = small.tile([P, M_HALVES], F32)
+            for h in range(M_HALVES):
+                nc.tensor.matmul(
+                    out=s_ps[h][:],
+                    lhsT=q_sb[:, i * P : (i + 1) * P],
+                    rhs=k_sb[:, h * BANK : (h + 1) * BANK],
+                    start=True,
+                    stop=True,
+                )
+                nc.vector.reduce_max(out=half_max[:, h : h + 1], in_=s_ps[h][:], axis=AX.X)
+            minus_max = small.tile([P, 1], F32)
+            nc.vector.tensor_scalar(
+                out=minus_max[:],
+                in0=half_max[:, 0:1],
+                scalar1=half_max[:, 1:2],
+                scalar2=-1.0,
+                op0=ALU.max,
+                op1=ALU.mult,
+            )
+            e_sb = work.tile([P, M_POS], BF16)
+            for h in range(M_HALVES):
+                nc.scalar.activation(
+                    out=e_sb[:, h * BANK : (h + 1) * BANK],
+                    in_=s_ps[h][:],
+                    func=ACT.Exp,
+                    bias=minus_max[:],
+                    scale=1.0,
+                    accum_out=row_sums[group][:, j, h : h + 1],
+                )
+            e_rows[i] = e_sb
+
+        def turn_e(i):
+            grouped = work.tile([P, M_PASSES, P, PACK], BF16, align_bytes=64, name="e_grouped")
+            blocks = [e_rows[i][:, b * P : (b + 1) * P] for b in range(M_PASSES * PACK)]
+            transpose_and_group(blocks, grouped[:])
+            e_grouped[i] = grouped
+
+        def quantise_e(i):
+            words = codes.tile([P, M_PASSES, P], U32, align_bytes=64, name="e_words")
+            scales = codes.tile([P, M_PASSES, P], U8, align_bytes=64, name="e_scales")
+            nc.vector.quantize_mx(
+                out=words[:].rearrange("p g n -> p (g n)").bitcast(FP8X4),
+                scales=scales[:].rearrange("p g n -> p (g n)"),
+                in_=e_grouped[i][:].rearrange("p g n t -> p (g n t)"),
+            )
+            e_packed[i] = (words, scales)
+
+        def spread_inverse_sums(group):
+            sums = small.tile([P, GROUP], F32)
+            nc.vector.reduce_sum(out=sums[:], in_=row_sums[group][:], axis=AX.X)
+            inverse = small.tile([P, GROUP], F32)
+            nc.vector.reciprocal(out=inverse[:], in_=sums[:])
+            repeated = pair.tile([P, GROUP, P], F32)
+            nc.gpsimd.tensor_scalar(
+                out=repeated[:],
+                in0=inverse[:].unsqueeze(2).to_broadcast([P, GROUP, P]),
+                scalar1=1.0,
+                scalar2=0.0,
+                op0=ALU.mult,
+                op1=ALU.add,
+            )
+            turned = psum_o.tile([P, GROUP, P], F32, tag="o")
+            for j in range(GROUP):
+                nc.tensor.transpose(turned[:, j, :], repeated[:, j, :], ident_f32[:])
+            spread = pair.tile([P, GROUP, P], F32)
+            nc.scalar.copy(out=spread[:], in_=turned[:])
+            inverse_sums[group] = spread
+
+        def attend(i):
+            group, j = divmod(i, GROUP)
+            if j == 0:
+                att_grouped[group] = pair.tile([P, GROUP, P, PACK], BF16, align_bytes=64, name="att_grouped")
+            words, scales = e_packed[i]
+            att_ps = psum_o.tile([P, PACK, P], F32, tag="o")
+            for t in range(PACK):
+                for g in range(M_PASSES):
+                    nc.tensor.matmul_mx(
+                        out=att_ps[:, t, :],
+                        lhsT=v_words[:, g, t * P : (t + 1) * P].bitcast(FP8X4),
+                        lhsT_scale=v_scales[:, g, t * P : (t + 1) * P],
+                        rhs=words[:, g, :].bitcast(FP8X4),
+                        rhs_scale=scales[:, g, :],
+                        start=(g == 0),
+                        stop=(g == M_PASSES - 1),
+                    )
+            nc.vector.tensor_tensor(
+                out=att_grouped[group][:, j, :, :],
+                in0=att_ps[:].rearrange("p t n -> p n t"),
+                in1=inverse_sums[group][:, j, :].unsqueeze(2).to_broadcast([P, P, PACK]),
+                op=ALU.mult,
+            )
+
+        def project(group):
+            words = pair.tile([P, GROUP * P], U32, align_bytes=64, name="att_words")
+            scales = pair.tile([P, GROUP * P], U8, align_bytes=64, name="att_scales")
+            nc.vector.quantize_mx(
+                out=words[:].bitcast(FP8X4),
+                scales=scales[:],
+                in_=att_grouped[group][:].rearrange("p j n t -> p (j n t)"),
+            )
+            cols = slice(group * GROUP * P, (group + 1) * GROUP * P)
+            for c in range(CHUNKS):
+                y_ps = psum_o.tile([P, BANK], F32, tag="o")
+                nc.tensor.matmul_mx(
+                    out=y_ps[:],
+                    lhsT=w_words[:, 0, c * P : (c + 1) * P].bitcast(FP8X4),
+                    lhsT_scale=w_scales[:, 0, c * P : (c + 1) * P],
+                    rhs=words[:].bitcast(FP8X4),
+                    rhs_scale=scales[:],
+                    start=True,
+                    stop=True,
+                )
+                result = stores.tile([P, BANK], F32)
+                nc.vector.scalar_tensor_tensor(
+                    out=result[:],
+                    in0=y_ps[:],
+                    scalar=gain_f32[:, 0:1],
+                    in1=imgs_sb[:, c, cols],
+                    op0=ALU.mult,
+                    op1=ALU.add,
+                )
+                nc.sync.dma_start(out=out_view[:, c, cols], in_=result[:])
+
+        TURN_LAG = 1
+        QUANTISE_LAG = 2
+        ATTEND_LAG = GROUP + 1
+        for step in range(TILES + ATTEND_LAG):
+            if step < TILES:
+                scores_and_exp(step)
+            if 0 <= step - TURN_LAG < TILES:
+                turn_e(step - TURN_LAG)
+            if 0 <= step - QUANTISE_LAG < TILES:
+                quantise_e(step - QUANTISE_LAG)
+            if step < TILES and step % GROUP == GROUP - 1:
+                spread_inverse_sums(step // GROUP)
+            if step >= ATTEND_LAG:
+                attend(step - ATTEND_LAG)
+                if (step - ATTEND_LAG) % GROUP == GROUP - 1:
+                    project((step - ATTEND_LAG) // GROUP)

@@ -34,13 +34,13 @@ def tile_selfattentionconv2d_pb_t_kernel(tc, q, k_pool, v_pool, imgs, w_out, gai
     with ExitStack() as ctx:
         keep = ctx.enter_context(tc.tile_pool(name="keep", bufs=1))
         small = ctx.enter_context(tc.tile_pool(name="small", bufs=4))
-        work = ctx.enter_context(tc.tile_pool(name="work", bufs=3))
+        work = ctx.enter_context(tc.tile_pool(name="work", bufs=4))
         codes = ctx.enter_context(tc.tile_pool(name="codes", bufs=7))
         pair = ctx.enter_context(tc.tile_pool(name="pair", bufs=2))
         stores = ctx.enter_context(tc.tile_pool(name="stores", bufs=4))
         psum_s = ctx.enter_context(tc.psum_pool(name="psum_s", bufs=4))
         psum_t = ctx.enter_context(tc.psum_pool(name="psum_t", bufs=2))
-        psum_o = ctx.enter_context(tc.psum_pool(name="psum_o", bufs=2))
+        psum_w = ctx.enter_context(tc.psum_pool(name="psum_w", bufs=2))
 
         q_sb = keep.tile([P, N_PIX], BF16)
         k_sb = keep.tile([P, M_POS], BF16)
@@ -51,14 +51,15 @@ def tile_selfattentionconv2d_pb_t_kernel(tc, q, k_pool, v_pool, imgs, w_out, gai
         q_view = q.rearrange("b d n -> (b d) n")
         imgs_view = imgs.rearrange("b (c p) h w -> p (b c) (h w)", p=P)
         out_view = out.rearrange("b (c p) h w -> p (b c) (h w)", p=P)
-        quarter = N_PIX // 4
-        nc.sync.dma_start(out=k_sb[:], in_=k_pool.rearrange("b d m -> (b d) m"))
-        nc.sync.dma_start(out=q_sb[:, 0:quarter], in_=q_view[:, 0:quarter])
+        k_view = k_pool.rearrange("b d m -> (b d) m")
+        first = GROUP * P
+        nc.sync.dma_start(out=q_sb[:, 0:first], in_=q_view[:, 0:first])
+        for h in range(M_HALVES):
+            nc.sync.dma_start(out=k_sb[:, h * BANK : (h + 1) * BANK], in_=k_view[:, h * BANK : (h + 1) * BANK])
         nc.sync.dma_start(out=v_sb[:], in_=v_pool.rearrange("b (c p) m -> p (b c) m", p=P))
-        for piece in range(1, 4):
-            cols = slice(piece * quarter, (piece + 1) * quarter)
-            nc.sync.dma_start(out=q_sb[:, cols], in_=q_view[:, cols])
+        nc.sync.dma_start(out=q_sb[:, first : N_PIX // 2], in_=q_view[:, first : N_PIX // 2])
         nc.sync.dma_start(out=w_sb[:], in_=w_out.rearrange("(c p) d -> p c d", p=P))
+        nc.sync.dma_start(out=q_sb[:, N_PIX // 2 : N_PIX], in_=q_view[:, N_PIX // 2 : N_PIX])
         nc.scalar.dma_start(out=gain_bf[:], in_=gain.partition_broadcast(P))
         for c in range(CHUNKS):
             nc.sync.dma_start(out=imgs_sb[:, c, :], in_=imgs_view[:, c, :])
@@ -70,58 +71,77 @@ def tile_selfattentionconv2d_pb_t_kernel(tc, q, k_pool, v_pool, imgs, w_out, gai
         gain_f32 = keep.tile([P, 1], F32)
         nc.vector.tensor_copy(out=gain_f32[:], in_=gain_bf[:])
 
-        def transpose_and_group(blocks, grouped):
-            turned = psum_t.tile([P, 2 * PACK, P], BF16, tag="turned")
+        def transpose_blocks(blocks, turned):
             for index, block in enumerate(blocks):
                 nc.tensor.transpose(turned[:, index, :], block, ident_bf[:])
-            nc.scalar.copy(out=grouped, in_=turned[:].rearrange("p (r t) n -> p r n t", t=PACK))
 
-        def quantise_weights(rows_sb, passes, name):
-            grouped = keep.tile([P, passes, CHUNKS * P, PACK], BF16, align_bytes=64, name=name + "_grouped")
-            words = keep.tile([P, passes, CHUNKS * P], U32, align_bytes=64, name=name + "_words")
-            scales = keep.tile([P, passes, CHUNKS * P], U8, align_bytes=64, name=name + "_scales")
-            for g in range(passes):
-                for half in range(CHUNKS // 2):
-                    blocks = [
-                        rows_sb[:, 2 * half + r, (PACK * g + t) * P : (PACK * g + t + 1) * P]
-                        for r in range(2)
-                        for t in range(PACK)
-                    ]
-                    rows = slice(2 * half * P, (2 * half + 2) * P)
-                    transpose_and_group(blocks, grouped[:, g, rows, :].rearrange("p (r n) t -> p r n t", r=2))
-            for g in range(passes):
-                nc.vector.quantize_mx(
-                    out=words[:, g, :].bitcast(FP8X4),
-                    scales=scales[:, g, :],
-                    in_=grouped[:, g, :, :].rearrange("p n t -> p (n t)"),
-                )
-            return words, scales
+        def group_by_word(turned, grouped, copy_out):
+            copy_out(out=grouped, in_=turned[:].rearrange("p (r t) n -> p r n t", t=PACK))
 
-        v_words, v_scales = quantise_weights(v_sb, M_PASSES, "v")
-        w_words, w_scales = quantise_weights(w_sb, 1, "w")
+        v_grouped = keep.tile([P, M_PASSES, DV, PACK], BF16, align_bytes=64)
+        v_words = keep.tile([P, M_PASSES, DV], U32, align_bytes=64)
+        v_scales = keep.tile([P, M_PASSES, DV], U8, align_bytes=64)
+        w_grouped = keep.tile([P, 1, C_OUT, PACK], BF16, align_bytes=64)
+        w_words = keep.tile([P, 1, C_OUT], U32, align_bytes=64)
+        w_scales = keep.tile([P, 1, C_OUT], U8, align_bytes=64)
+        weights_sb = {"v": v_sb, "w": w_sb}
+        weights_grouped = {"v": v_grouped, "w": w_grouped}
 
+        weights_turned = {}
+
+        def turn_weights(matrix, g, half):
+            rows_sb = weights_sb[matrix]
+            blocks = [
+                rows_sb[:, 2 * half + r, (PACK * g + t) * P : (PACK * g + t + 1) * P]
+                for r in range(2)
+                for t in range(PACK)
+            ]
+            turned = psum_w.tile([P, 2 * PACK, P], BF16, tag="wide")
+            transpose_blocks(blocks, turned)
+            weights_turned[(matrix, g, half)] = turned
+
+        def group_weights(matrix, g, half):
+            rows = slice(2 * half * P, (2 * half + 2) * P)
+            group_by_word(
+                weights_turned[(matrix, g, half)],
+                weights_grouped[matrix][:, g, rows, :].rearrange("p (r n) t -> p r n t", r=2),
+                nc.vector.tensor_copy,
+            )
+
+        def quantise_weights(grouped, words, scales, g):
+            nc.vector.quantize_mx(
+                out=words[:, g, :].bitcast(FP8X4),
+                scales=scales[:, g, :],
+                in_=grouped[:, g, :, :].rearrange("p n t -> p (n t)"),
+            )
+
+        s_banks = {}
+        minus_maxima = {}
         e_rows = {}
         e_grouped = {}
         e_packed = {}
         row_sums = {}
         inverse_sums = {}
+        att_banks = {}
         att_grouped = {}
+        att_packed = {}
+        y_banks = {}
 
-        def scores_and_exp(i):
-            group, j = divmod(i, GROUP)
-            if j == 0:
-                row_sums[group] = pair.tile([P, GROUP, M_HALVES], F32, name="row_sums")
-            s_ps = [psum_s.tile([P, BANK], F32, name="s_ps") for h in range(M_HALVES)]
-            half_max = small.tile([P, M_HALVES], F32)
+        def scores(i):
+            s_banks[i] = [psum_s.tile([P, BANK], F32, name="s_ps") for h in range(M_HALVES)]
             for h in range(M_HALVES):
                 nc.tensor.matmul(
-                    out=s_ps[h][:],
+                    out=s_banks[i][h][:],
                     lhsT=q_sb[:, i * P : (i + 1) * P],
                     rhs=k_sb[:, h * BANK : (h + 1) * BANK],
                     start=True,
                     stop=True,
                 )
-                nc.vector.reduce_max(out=half_max[:, h : h + 1], in_=s_ps[h][:], axis=AX.X)
+
+        def row_maximum(i):
+            half_max = small.tile([P, M_HALVES], F32)
+            for h in range(M_HALVES):
+                nc.vector.reduce_max(out=half_max[:, h : h + 1], in_=s_banks[i][h][:], axis=AX.X)
             minus_max = small.tile([P, 1], F32)
             nc.vector.tensor_scalar(
                 out=minus_max[:],
@@ -131,22 +151,29 @@ def tile_selfattentionconv2d_pb_t_kernel(tc, q, k_pool, v_pool, imgs, w_out, gai
                 op0=ALU.max,
                 op1=ALU.mult,
             )
+            minus_maxima[i] = minus_max
+
+        def exponentials(i):
+            group, j = divmod(i, GROUP)
+            if j == 0:
+                row_sums[group] = pair.tile([P, GROUP, M_HALVES], F32, name="row_sums")
             e_sb = work.tile([P, M_POS], BF16)
             for h in range(M_HALVES):
                 nc.scalar.activation(
                     out=e_sb[:, h * BANK : (h + 1) * BANK],
-                    in_=s_ps[h][:],
+                    in_=s_banks[i][h][:],
                     func=ACT.Exp,
-                    bias=minus_max[:],
+                    bias=minus_maxima[i][:],
                     scale=1.0,
                     accum_out=row_sums[group][:, j, h : h + 1],
                 )
             e_rows[i] = e_sb
 
         def turn_e(i):
+            turned = psum_t.tile([P, M_PASSES * PACK, P], BF16, tag="turned")
+            transpose_blocks([e_rows[i][:, b * P : (b + 1) * P] for b in range(M_PASSES * PACK)], turned)
             grouped = work.tile([P, M_PASSES, P, PACK], BF16, align_bytes=64, name="e_grouped")
-            blocks = [e_rows[i][:, b * P : (b + 1) * P] for b in range(M_PASSES * PACK)]
-            transpose_and_group(blocks, grouped[:])
+            group_by_word(turned, grouped[:], nc.scalar.copy)
             e_grouped[i] = grouped
 
         def quantise_e(i):
@@ -164,28 +191,22 @@ def tile_selfattentionconv2d_pb_t_kernel(tc, q, k_pool, v_pool, imgs, w_out, gai
             nc.vector.reduce_sum(out=sums[:], in_=row_sums[group][:], axis=AX.X)
             inverse = small.tile([P, GROUP], F32)
             nc.vector.reciprocal(out=inverse[:], in_=sums[:])
-            repeated = pair.tile([P, GROUP, P], F32)
-            nc.gpsimd.tensor_scalar(
-                out=repeated[:],
-                in0=inverse[:].unsqueeze(2).to_broadcast([P, GROUP, P]),
-                scalar1=1.0,
-                scalar2=0.0,
-                op0=ALU.mult,
-                op1=ALU.add,
-            )
-            turned = psum_o.tile([P, GROUP, P], F32, tag="o")
+            spread_ps = psum_t.tile([P, GROUP, P], F32, tag="turned")
             for j in range(GROUP):
-                nc.tensor.transpose(turned[:, j, :], repeated[:, j, :], ident_f32[:])
+                nc.tensor.matmul(
+                    out=spread_ps[:, j, :],
+                    lhsT=inverse[:, j : j + 1].to_broadcast([P, P]),
+                    rhs=ident_f32[:],
+                    start=True,
+                    stop=True,
+                )
             spread = pair.tile([P, GROUP, P], F32)
-            nc.scalar.copy(out=spread[:], in_=turned[:])
+            nc.scalar.copy(out=spread[:], in_=spread_ps[:])
             inverse_sums[group] = spread
 
         def attend(i):
-            group, j = divmod(i, GROUP)
-            if j == 0:
-                att_grouped[group] = pair.tile([P, GROUP, P, PACK], BF16, align_bytes=64, name="att_grouped")
             words, scales = e_packed[i]
-            att_ps = psum_o.tile([P, PACK, P], F32, tag="o")
+            att_ps = psum_w.tile([P, PACK, P], F32, tag="wide")
             for t in range(PACK):
                 for g in range(M_PASSES):
                     nc.tensor.matmul_mx(
@@ -197,57 +218,101 @@ def tile_selfattentionconv2d_pb_t_kernel(tc, q, k_pool, v_pool, imgs, w_out, gai
                         start=(g == 0),
                         stop=(g == M_PASSES - 1),
                     )
+            att_banks[i] = att_ps
+
+        def divide(i):
+            group, j = divmod(i, GROUP)
+            if j == 0:
+                att_grouped[group] = pair.tile([P, GROUP, P, PACK], BF16, align_bytes=64, name="att_grouped")
             nc.vector.tensor_tensor(
                 out=att_grouped[group][:, j, :, :],
-                in0=att_ps[:].rearrange("p t n -> p n t"),
+                in0=att_banks[i][:].rearrange("p t n -> p n t"),
                 in1=inverse_sums[group][:, j, :].unsqueeze(2).to_broadcast([P, P, PACK]),
                 op=ALU.mult,
             )
 
-        def project(group):
-            words = pair.tile([P, GROUP * P], U32, align_bytes=64, name="att_words")
-            scales = pair.tile([P, GROUP * P], U8, align_bytes=64, name="att_scales")
+        def quantise_att(i):
+            group, j = divmod(i, GROUP)
+            if j == 0:
+                att_packed[group] = (
+                    pair.tile([P, GROUP, P], U32, align_bytes=64, name="att_words"),
+                    pair.tile([P, GROUP, P], U8, align_bytes=64, name="att_scales"),
+                )
+            words, scales = att_packed[group]
             nc.vector.quantize_mx(
-                out=words[:].bitcast(FP8X4),
-                scales=scales[:],
-                in_=att_grouped[group][:].rearrange("p j n t -> p (j n t)"),
+                out=words[:, j, :].bitcast(FP8X4),
+                scales=scales[:, j, :],
+                in_=att_grouped[group][:, j, :, :].rearrange("p n t -> p (n t)"),
             )
+
+        def project(group, c):
+            words, scales = att_packed[group]
+            y_ps = psum_w.tile([P, BANK], F32, tag="wide")
+            nc.tensor.matmul_mx(
+                out=y_ps[:],
+                lhsT=w_words[:, 0, c * P : (c + 1) * P].bitcast(FP8X4),
+                lhsT_scale=w_scales[:, 0, c * P : (c + 1) * P],
+                rhs=words[:].rearrange("p j n -> p (j n)").bitcast(FP8X4),
+                rhs_scale=scales[:].rearrange("p j n -> p (j n)"),
+                start=True,
+                stop=True,
+            )
+            y_banks[(group, c)] = y_ps
+
+        def finish(group, c):
             cols = slice(group * GROUP * P, (group + 1) * GROUP * P)
-            for c in range(CHUNKS):
-                y_ps = psum_o.tile([P, BANK], F32, tag="o")
-                nc.tensor.matmul_mx(
-                    out=y_ps[:],
-                    lhsT=w_words[:, 0, c * P : (c + 1) * P].bitcast(FP8X4),
-                    lhsT_scale=w_scales[:, 0, c * P : (c + 1) * P],
-                    rhs=words[:].bitcast(FP8X4),
-                    rhs_scale=scales[:],
-                    start=True,
-                    stop=True,
-                )
-                result = stores.tile([P, BANK], F32)
-                nc.vector.scalar_tensor_tensor(
-                    out=result[:],
-                    in0=y_ps[:],
-                    scalar=gain_f32[:, 0:1],
-                    in1=imgs_sb[:, c, cols],
-                    op0=ALU.mult,
-                    op1=ALU.add,
-                )
-                nc.sync.dma_start(out=out_view[:, c, cols], in_=result[:])
+            result = stores.tile([P, BANK], F32)
+            nc.vector.scalar_tensor_tensor(
+                out=result[:],
+                in0=y_banks[(group, c)][:],
+                scalar=gain_f32[:, 0:1],
+                in1=imgs_sb[:, c, cols],
+                op0=ALU.mult,
+                op1=ALU.add,
+            )
+            nc.sync.dma_start(out=out_view[:, c, cols], in_=result[:])
 
         TURN_LAG = 1
-        QUANTISE_LAG = 2
+        QUANTISE_LAG = 3
+        SUMS_LAG = 1
         ATTEND_LAG = GROUP + 1
-        for step in range(TILES + ATTEND_LAG):
-            if step < TILES:
-                scores_and_exp(step)
-            if 0 <= step - TURN_LAG < TILES:
-                turn_e(step - TURN_LAG)
-            if 0 <= step - QUANTISE_LAG < TILES:
-                quantise_e(step - QUANTISE_LAG)
-            if step < TILES and step % GROUP == GROUP - 1:
-                spread_inverse_sums(step // GROUP)
-            if step >= ATTEND_LAG:
-                attend(step - ATTEND_LAG)
-                if (step - ATTEND_LAG) % GROUP == GROUP - 1:
-                    project((step - ATTEND_LAG) // GROUP)
+        DIVIDE_LAG = ATTEND_LAG + 1
+        PROJECT_LAG = DIVIDE_LAG + GROUP - 1
+        FINISH_LAG = PROJECT_LAG + 1
+        assert CHUNKS == GROUP
+        v_pieces = [("v", g, half) for g in range(M_PASSES) for half in range(CHUNKS // 2)]
+        w_pieces = [("w", 0, half) for half in range(CHUNKS // 2)]
+        weight_pieces = v_pieces + w_pieces
+        with tc.manual_schedule():
+            scores(0)
+            for step in range(TILES + FINISH_LAG):
+                if step < TILES:
+                    row_maximum(step)
+                    exponentials(step)
+                if step + 1 < TILES:
+                    scores(step + 1)
+                if 0 <= step - TURN_LAG < TILES:
+                    turn_e(step - TURN_LAG)
+                if 0 <= step - 1 < len(weight_pieces):
+                    group_weights(*weight_pieces[step - 1])
+                if step < len(weight_pieces):
+                    turn_weights(*weight_pieces[step])
+                if 0 <= step - DIVIDE_LAG < TILES:
+                    divide(step - DIVIDE_LAG)
+                if 0 <= step - ATTEND_LAG < TILES:
+                    attend(step - ATTEND_LAG)
+                if step >= FINISH_LAG:
+                    finish(*divmod(step - FINISH_LAG, CHUNKS))
+                if 0 <= step - QUANTISE_LAG < TILES:
+                    quantise_e(step - QUANTISE_LAG)
+                if step == len(v_pieces):
+                    for g in range(M_PASSES):
+                        quantise_weights(v_grouped, v_words, v_scales, g)
+                if step == len(weight_pieces):
+                    quantise_weights(w_grouped, w_words, w_scales, 0)
+                if 0 <= step - DIVIDE_LAG < TILES:
+                    quantise_att(step - DIVIDE_LAG)
+                if 0 <= step - PROJECT_LAG < TILES:
+                    project(*divmod(step - PROJECT_LAG, CHUNKS))
+                if 0 <= step - SUMS_LAG < TILES and (step - SUMS_LAG) % GROUP == GROUP - 1:
+                    spread_inverse_sums((step - SUMS_LAG) // GROUP)

@@ -283,36 +283,35 @@ def tile_selfattentionconv2d_pb_t_kernel(tc, q, k_pool, v_pool, imgs, w_out, gai
         v_pieces = [("v", g, half) for g in range(M_PASSES) for half in range(CHUNKS // 2)]
         w_pieces = [("w", 0, half) for half in range(CHUNKS // 2)]
         weight_pieces = v_pieces + w_pieces
-        with tc.manual_schedule():
-            scores(0)
-            for step in range(TILES + FINISH_LAG):
-                if step < TILES:
-                    row_maximum(step)
-                    exponentials(step)
-                if step + 1 < TILES:
-                    scores(step + 1)
-                if 0 <= step - TURN_LAG < TILES:
-                    turn_e(step - TURN_LAG)
-                if 0 <= step - 1 < len(weight_pieces):
-                    group_weights(*weight_pieces[step - 1])
-                if step < len(weight_pieces):
-                    turn_weights(*weight_pieces[step])
-                if 0 <= step - DIVIDE_LAG < TILES:
-                    divide(step - DIVIDE_LAG)
-                if 0 <= step - ATTEND_LAG < TILES:
-                    attend(step - ATTEND_LAG)
-                if step >= FINISH_LAG:
-                    finish(*divmod(step - FINISH_LAG, CHUNKS))
-                if 0 <= step - QUANTISE_LAG < TILES:
-                    quantise_e(step - QUANTISE_LAG)
-                if step == len(v_pieces):
-                    for g in range(M_PASSES):
-                        quantise_weights(v_grouped, v_words, v_scales, g)
-                if step == len(weight_pieces):
-                    quantise_weights(w_grouped, w_words, w_scales, 0)
-                if 0 <= step - DIVIDE_LAG < TILES:
-                    quantise_att(step - DIVIDE_LAG)
-                if 0 <= step - PROJECT_LAG < TILES:
-                    project(*divmod(step - PROJECT_LAG, CHUNKS))
-                if 0 <= step - SUMS_LAG < TILES and (step - SUMS_LAG) % GROUP == GROUP - 1:
-                    spread_inverse_sums((step - SUMS_LAG) // GROUP)
+        scores(0)
+        for step in range(TILES + FINISH_LAG):
+            if step < TILES:
+                row_maximum(step)
+                exponentials(step)
+            if step + 1 < TILES:
+                scores(step + 1)
+            if 0 <= step - TURN_LAG < TILES:
+                turn_e(step - TURN_LAG)
+            if 0 <= step - 1 < len(weight_pieces):
+                group_weights(*weight_pieces[step - 1])
+            if step < len(weight_pieces):
+                turn_weights(*weight_pieces[step])
+            if 0 <= step - DIVIDE_LAG < TILES:
+                divide(step - DIVIDE_LAG)
+            if 0 <= step - ATTEND_LAG < TILES:
+                attend(step - ATTEND_LAG)
+            if step >= FINISH_LAG:
+                finish(*divmod(step - FINISH_LAG, CHUNKS))
+            if 0 <= step - QUANTISE_LAG < TILES:
+                quantise_e(step - QUANTISE_LAG)
+            if step == len(v_pieces):
+                for g in range(M_PASSES):
+                    quantise_weights(v_grouped, v_words, v_scales, g)
+            if step == len(weight_pieces):
+                quantise_weights(w_grouped, w_words, w_scales, 0)
+            if 0 <= step - DIVIDE_LAG < TILES:
+                quantise_att(step - DIVIDE_LAG)
+            if 0 <= step - PROJECT_LAG < TILES:
+                project(*divmod(step - PROJECT_LAG, CHUNKS))
+            if 0 <= step - SUMS_LAG < TILES and (step - SUMS_LAG) % GROUP == GROUP - 1:
+                spread_inverse_sums((step - SUMS_LAG) // GROUP)

@@ -14,17 +14,27 @@ AX = mybir.AxisListType
 
 P = 128
 PACK = 4
-BANK = 512
+PAIR = 2
+K_PASS = P * PACK
 N_PIX = 4096
 M_POS = 1024
 DV = 512
 C_OUT = 512
-M_PASSES = M_POS // (P * PACK)
-M_HALVES = M_POS // BANK
+M_PASSES = M_POS // K_PASS
 TILES = N_PIX // P
-GROUP = 4
+GROUP = K_PASS // P
 GROUPS = TILES // GROUP
-CHUNKS = 4
+CHUNKS = DV // P
+assert DV == K_PASS and C_OUT == DV and CHUNKS == GROUP == PACK
+assert M_PASSES == 2
+
+TURN_LAG = 1
+QUANTISE_LAG = 3
+SUMS_LAG = 1
+ATTEND_LAG = GROUP + 1
+DIVIDE_LAG = ATTEND_LAG + 1
+PROJECT_LAG = DIVIDE_LAG + GROUP - 1
+FINISH_LAG = PROJECT_LAG + 1
 
 FLOPS = 2 * N_PIX * M_POS * P + 2 * N_PIX * M_POS * DV + 2 * N_PIX * DV * C_OUT
 
@@ -34,13 +44,13 @@ def tile_selfattentionconv2d_pb_t_kernel(tc, q, k_pool, v_pool, imgs, w_out, gai
     with ExitStack() as ctx:
         keep = ctx.enter_context(tc.tile_pool(name="keep", bufs=1))
         small = ctx.enter_context(tc.tile_pool(name="small", bufs=4))
-        work = ctx.enter_context(tc.tile_pool(name="work", bufs=4))
-        codes = ctx.enter_context(tc.tile_pool(name="codes", bufs=7))
-        pair = ctx.enter_context(tc.tile_pool(name="pair", bufs=2))
+        work = ctx.enter_context(tc.tile_pool(name="work", bufs=QUANTISE_LAG + 1))
+        codes = ctx.enter_context(tc.tile_pool(name="codes", bufs=ATTEND_LAG - QUANTISE_LAG + 2))
+        by_group = ctx.enter_context(tc.tile_pool(name="by_group", bufs=2))
         stores = ctx.enter_context(tc.tile_pool(name="stores", bufs=4))
-        psum_s = ctx.enter_context(tc.psum_pool(name="psum_s", bufs=4))
+        psum_s = ctx.enter_context(tc.psum_pool(name="psum_s", bufs=2 * M_PASSES))
         psum_t = ctx.enter_context(tc.psum_pool(name="psum_t", bufs=2))
-        psum_w = ctx.enter_context(tc.psum_pool(name="psum_w", bufs=2))
+        psum_o = ctx.enter_context(tc.psum_pool(name="psum_o", bufs=2))
 
         q_sb = keep.tile([P, N_PIX], BF16)
         k_sb = keep.tile([P, M_POS], BF16)
@@ -49,14 +59,16 @@ def tile_selfattentionconv2d_pb_t_kernel(tc, q, k_pool, v_pool, imgs, w_out, gai
         imgs_sb = keep.tile([P, CHUNKS, N_PIX], BF16)
         gain_bf = keep.tile([P, 1], BF16)
         q_view = q.rearrange("b d n -> (b d) n")
+        k_view = k_pool.rearrange("b d m -> (b d) m")
         imgs_view = imgs.rearrange("b (c p) h w -> p (b c) (h w)", p=P)
         out_view = out.rearrange("b (c p) h w -> p (b c) (h w)", p=P)
-        k_view = k_pool.rearrange("b d m -> (b d) m")
         first = GROUP * P
         nc.sync.dma_start(out=q_sb[:, 0:first], in_=q_view[:, 0:first])
-        for h in range(M_HALVES):
-            nc.sync.dma_start(out=k_sb[:, h * BANK : (h + 1) * BANK], in_=k_view[:, h * BANK : (h + 1) * BANK])
-        nc.sync.dma_start(out=v_sb[:], in_=v_pool.rearrange("b (c p) m -> p (b c) m", p=P))
+        for g in range(M_PASSES):
+            nc.sync.dma_start(out=k_sb[:, g * K_PASS : (g + 1) * K_PASS], in_=k_view[:, g * K_PASS : (g + 1) * K_PASS])
+        v_view = v_pool.rearrange("b (u p e) m -> p (b u) e m", u=PAIR, e=PAIR)
+        for u in range(PAIR):
+            nc.sync.dma_start(out=v_sb[:, PAIR * u : PAIR * (u + 1), :], in_=v_view[:, u, :, :])
         nc.sync.dma_start(out=q_sb[:, first : N_PIX // 2], in_=q_view[:, first : N_PIX // 2])
         nc.sync.dma_start(out=w_sb[:], in_=w_out.rearrange("(c p) d -> p c d", p=P))
         nc.sync.dma_start(out=q_sb[:, N_PIX // 2 : N_PIX], in_=q_view[:, N_PIX // 2 : N_PIX])
@@ -71,49 +83,44 @@ def tile_selfattentionconv2d_pb_t_kernel(tc, q, k_pool, v_pool, imgs, w_out, gai
         gain_f32 = keep.tile([P, 1], F32)
         nc.vector.tensor_copy(out=gain_f32[:], in_=gain_bf[:])
 
-        def transpose_blocks(blocks, turned):
-            for index, block in enumerate(blocks):
-                nc.tensor.transpose(turned[:, index, :], block, ident_bf[:])
-
-        def group_by_word(turned, grouped, copy_out):
-            copy_out(out=grouped, in_=turned[:].rearrange("p (r t) n -> p r n t", t=PACK))
-
-        v_grouped = keep.tile([P, M_PASSES, DV, PACK], BF16, align_bytes=64)
-        v_words = keep.tile([P, M_PASSES, DV], U32, align_bytes=64)
-        v_scales = keep.tile([P, M_PASSES, DV], U8, align_bytes=64)
-        w_grouped = keep.tile([P, 1, C_OUT, PACK], BF16, align_bytes=64)
-        w_words = keep.tile([P, 1, C_OUT], U32, align_bytes=64)
-        w_scales = keep.tile([P, 1, C_OUT], U8, align_bytes=64)
         weights_sb = {"v": v_sb, "w": w_sb}
-        weights_grouped = {"v": v_grouped, "w": w_grouped}
-
+        weights_passes = {"v": M_PASSES, "w": 1}
+        weights_grouped = {}
+        weights_words = {}
+        weights_scales = {}
+        for matrix in ("v", "w"):
+            shape = [P, weights_passes[matrix], CHUNKS * P]
+            weights_grouped[matrix] = keep.tile(shape + [PACK], BF16, align_bytes=64, name=matrix + "_grouped")
+            weights_words[matrix] = keep.tile(shape, U32, align_bytes=64, name=matrix + "_words")
+            weights_scales[matrix] = keep.tile(shape, U8, align_bytes=64, name=matrix + "_scales")
         weights_turned = {}
 
         def turn_weights(matrix, g, half):
-            rows_sb = weights_sb[matrix]
-            blocks = [
-                rows_sb[:, 2 * half + r, (PACK * g + t) * P : (PACK * g + t + 1) * P]
-                for r in range(2)
-                for t in range(PACK)
-            ]
-            turned = psum_w.tile([P, 2 * PACK, P], BF16, tag="wide")
-            transpose_blocks(blocks, turned)
+            turned = psum_o.tile([P, PAIR * PAIR, P], F32, tag="o")
+            for r in range(PAIR):
+                row_words = weights_sb[matrix][:, PAIR * half + r, :].bitcast(F32)
+                for u in range(PAIR):
+                    first_word = (PAIR * g + u) * P
+                    nc.tensor.transpose(
+                        turned[:, PAIR * r + u, :], row_words[:, first_word : first_word + P], ident_f32[:]
+                    )
             weights_turned[(matrix, g, half)] = turned
 
         def group_weights(matrix, g, half):
-            rows = slice(2 * half * P, (2 * half + 2) * P)
-            group_by_word(
-                weights_turned[(matrix, g, half)],
-                weights_grouped[matrix][:, g, rows, :].rearrange("p (r n) t -> p r n t", r=2),
-                nc.vector.tensor_copy,
+            rows = slice(PAIR * half * P, PAIR * (half + 1) * P)
+            grouped_words = weights_grouped[matrix][:, g, rows, :].rearrange("p n t -> p (n t)").bitcast(F32)
+            nc.vector.tensor_copy(
+                out=grouped_words.rearrange("p (r n u) -> p r n u", r=PAIR, u=PAIR),
+                in_=weights_turned[(matrix, g, half)][:].rearrange("p (r u) n -> p r n u", u=PAIR),
             )
 
-        def quantise_weights(grouped, words, scales, g):
-            nc.vector.quantize_mx(
-                out=words[:, g, :].bitcast(FP8X4),
-                scales=scales[:, g, :],
-                in_=grouped[:, g, :, :].rearrange("p n t -> p (n t)"),
-            )
+        def quantise_weights(matrix):
+            for g in range(weights_passes[matrix]):
+                nc.vector.quantize_mx(
+                    out=weights_words[matrix][:, g, :].bitcast(FP8X4),
+                    scales=weights_scales[matrix][:, g, :],
+                    in_=weights_grouped[matrix][:, g, :, :].rearrange("p n t -> p (n t)"),
+                )
 
         s_banks = {}
         minus_maxima = {}
@@ -128,25 +135,25 @@ def tile_selfattentionconv2d_pb_t_kernel(tc, q, k_pool, v_pool, imgs, w_out, gai
         y_banks = {}
 
         def scores(i):
-            s_banks[i] = [psum_s.tile([P, BANK], F32, name="s_ps") for h in range(M_HALVES)]
-            for h in range(M_HALVES):
+            s_banks[i] = [psum_s.tile([P, K_PASS], F32, name="s_ps") for g in range(M_PASSES)]
+            for g in range(M_PASSES):
                 nc.tensor.matmul(
-                    out=s_banks[i][h][:],
+                    out=s_banks[i][g][:],
                     lhsT=q_sb[:, i * P : (i + 1) * P],
-                    rhs=k_sb[:, h * BANK : (h + 1) * BANK],
+                    rhs=k_sb[:, g * K_PASS : (g + 1) * K_PASS],
                     start=True,
                     stop=True,
                 )
 
         def row_maximum(i):
-            half_max = small.tile([P, M_HALVES], F32)
-            for h in range(M_HALVES):
-                nc.vector.reduce_max(out=half_max[:, h : h + 1], in_=s_banks[i][h][:], axis=AX.X)
+            bank_max = small.tile([P, M_PASSES], F32)
+            for g in range(M_PASSES):
+                nc.vector.reduce_max(out=bank_max[:, g : g + 1], in_=s_banks[i][g][:], axis=AX.X)
             minus_max = small.tile([P, 1], F32)
             nc.vector.tensor_scalar(
                 out=minus_max[:],
-                in0=half_max[:, 0:1],
-                scalar1=half_max[:, 1:2],
+                in0=bank_max[:, 0:1],
+                scalar1=bank_max[:, 1:2],
                 scalar2=-1.0,
                 op0=ALU.max,
                 op1=ALU.mult,
@@ -156,24 +163,25 @@ def tile_selfattentionconv2d_pb_t_kernel(tc, q, k_pool, v_pool, imgs, w_out, gai
         def exponentials(i):
             group, j = divmod(i, GROUP)
             if j == 0:
-                row_sums[group] = pair.tile([P, GROUP, M_HALVES], F32, name="row_sums")
+                row_sums[group] = by_group.tile([P, GROUP, M_PASSES], F32, name="row_sums")
             e_sb = work.tile([P, M_POS], BF16)
-            for h in range(M_HALVES):
+            for g in range(M_PASSES):
                 nc.scalar.activation(
-                    out=e_sb[:, h * BANK : (h + 1) * BANK],
-                    in_=s_banks[i][h][:],
+                    out=e_sb[:, g * K_PASS : (g + 1) * K_PASS].rearrange("n (u e p) -> n u e p", u=PAIR, e=PAIR),
+                    in_=s_banks[i][g][:].rearrange("n (u p e) -> n u e p", u=PAIR, e=PAIR),
                     func=ACT.Exp,
                     bias=minus_maxima[i][:],
                     scale=1.0,
-                    accum_out=row_sums[group][:, j, h : h + 1],
+                    accum_out=row_sums[group][:, j, g : g + 1],
                 )
             e_rows[i] = e_sb
 
         def turn_e(i):
-            turned = psum_t.tile([P, M_PASSES * PACK, P], BF16, tag="turned")
-            transpose_blocks([e_rows[i][:, b * P : (b + 1) * P] for b in range(M_PASSES * PACK)], turned)
+            turned = psum_t.tile([P, M_PASSES * PACK, P], BF16, tag="t")
+            for block in range(M_PASSES * PACK):
+                nc.tensor.transpose(turned[:, block, :], e_rows[i][:, block * P : (block + 1) * P], ident_bf[:])
             grouped = work.tile([P, M_PASSES, P, PACK], BF16, align_bytes=64, name="e_grouped")
-            group_by_word(turned, grouped[:], nc.scalar.copy)
+            nc.scalar.copy(out=grouped[:], in_=turned[:].rearrange("p (g t) n -> p g n t", t=PACK))
             e_grouped[i] = grouped
 
         def quantise_e(i):
@@ -191,7 +199,7 @@ def tile_selfattentionconv2d_pb_t_kernel(tc, q, k_pool, v_pool, imgs, w_out, gai
             nc.vector.reduce_sum(out=sums[:], in_=row_sums[group][:], axis=AX.X)
             inverse = small.tile([P, GROUP], F32)
             nc.vector.reciprocal(out=inverse[:], in_=sums[:])
-            spread_ps = psum_t.tile([P, GROUP, P], F32, tag="turned")
+            spread_ps = psum_t.tile([P, GROUP, P], F32, tag="t")
             for j in range(GROUP):
                 nc.tensor.matmul(
                     out=spread_ps[:, j, :],
@@ -200,19 +208,19 @@ def tile_selfattentionconv2d_pb_t_kernel(tc, q, k_pool, v_pool, imgs, w_out, gai
                     start=True,
                     stop=True,
                 )
-            spread = pair.tile([P, GROUP, P], F32)
+            spread = by_group.tile([P, GROUP, P], F32)
             nc.scalar.copy(out=spread[:], in_=spread_ps[:])
             inverse_sums[group] = spread
 
         def attend(i):
             words, scales = e_packed[i]
-            att_ps = psum_w.tile([P, PACK, P], F32, tag="wide")
+            att_ps = psum_o.tile([P, PACK, P], F32, tag="o")
             for t in range(PACK):
                 for g in range(M_PASSES):
                     nc.tensor.matmul_mx(
                         out=att_ps[:, t, :],
-                        lhsT=v_words[:, g, t * P : (t + 1) * P].bitcast(FP8X4),
-                        lhsT_scale=v_scales[:, g, t * P : (t + 1) * P],
+                        lhsT=weights_words["v"][:, g, t * P : (t + 1) * P].bitcast(FP8X4),
+                        lhsT_scale=weights_scales["v"][:, g, t * P : (t + 1) * P],
                         rhs=words[:, g, :].bitcast(FP8X4),
                         rhs_scale=scales[:, g, :],
                         start=(g == 0),
@@ -223,7 +231,7 @@ def tile_selfattentionconv2d_pb_t_kernel(tc, q, k_pool, v_pool, imgs, w_out, gai
         def divide(i):
             group, j = divmod(i, GROUP)
             if j == 0:
-                att_grouped[group] = pair.tile([P, GROUP, P, PACK], BF16, align_bytes=64, name="att_grouped")
+                att_grouped[group] = by_group.tile([P, GROUP, P, PACK], BF16, align_bytes=64, name="att_grouped")
             nc.vector.tensor_tensor(
                 out=att_grouped[group][:, j, :, :],
                 in0=att_banks[i][:].rearrange("p t n -> p n t"),
@@ -235,8 +243,8 @@ def tile_selfattentionconv2d_pb_t_kernel(tc, q, k_pool, v_pool, imgs, w_out, gai
             group, j = divmod(i, GROUP)
             if j == 0:
                 att_packed[group] = (
-                    pair.tile([P, GROUP, P], U32, align_bytes=64, name="att_words"),
-                    pair.tile([P, GROUP, P], U8, align_bytes=64, name="att_scales"),
+                    by_group.tile([P, GROUP, P], U32, align_bytes=64, name="att_words"),
+                    by_group.tile([P, GROUP, P], U8, align_bytes=64, name="att_scales"),
                 )
             words, scales = att_packed[group]
             nc.vector.quantize_mx(
@@ -247,11 +255,11 @@ def tile_selfattentionconv2d_pb_t_kernel(tc, q, k_pool, v_pool, imgs, w_out, gai
 
         def project(group, c):
             words, scales = att_packed[group]
-            y_ps = psum_w.tile([P, BANK], F32, tag="wide")
+            y_ps = psum_o.tile([P, K_PASS], F32, tag="o")
             nc.tensor.matmul_mx(
                 out=y_ps[:],
-                lhsT=w_words[:, 0, c * P : (c + 1) * P].bitcast(FP8X4),
-                lhsT_scale=w_scales[:, 0, c * P : (c + 1) * P],
+                lhsT=weights_words["w"][:, 0, c * P : (c + 1) * P].bitcast(FP8X4),
+                lhsT_scale=weights_scales["w"][:, 0, c * P : (c + 1) * P],
                 rhs=words[:].rearrange("p j n -> p (j n)").bitcast(FP8X4),
                 rhs_scale=scales[:].rearrange("p j n -> p (j n)"),
                 start=True,
@@ -261,7 +269,7 @@ def tile_selfattentionconv2d_pb_t_kernel(tc, q, k_pool, v_pool, imgs, w_out, gai
 
         def finish(group, c):
             cols = slice(group * GROUP * P, (group + 1) * GROUP * P)
-            result = stores.tile([P, BANK], F32)
+            result = stores.tile([P, GROUP * P], F32)
             nc.vector.scalar_tensor_tensor(
                 out=result[:],
                 in0=y_banks[(group, c)][:],
@@ -272,16 +280,8 @@ def tile_selfattentionconv2d_pb_t_kernel(tc, q, k_pool, v_pool, imgs, w_out, gai
             )
             nc.sync.dma_start(out=out_view[:, c, cols], in_=result[:])
 
-        TURN_LAG = 1
-        QUANTISE_LAG = 3
-        SUMS_LAG = 1
-        ATTEND_LAG = GROUP + 1
-        DIVIDE_LAG = ATTEND_LAG + 1
-        PROJECT_LAG = DIVIDE_LAG + GROUP - 1
-        FINISH_LAG = PROJECT_LAG + 1
-        assert CHUNKS == GROUP
-        v_pieces = [("v", g, half) for g in range(M_PASSES) for half in range(CHUNKS // 2)]
-        w_pieces = [("w", 0, half) for half in range(CHUNKS // 2)]
+        v_pieces = [("v", g, half) for g in range(M_PASSES) for half in range(CHUNKS // PAIR)]
+        w_pieces = [("w", 0, half) for half in range(CHUNKS // PAIR)]
         weight_pieces = v_pieces + w_pieces
         scores(0)
         for step in range(TILES + FINISH_LAG):
@@ -305,10 +305,9 @@ def tile_selfattentionconv2d_pb_t_kernel(tc, q, k_pool, v_pool, imgs, w_out, gai
             if 0 <= step - QUANTISE_LAG < TILES:
                 quantise_e(step - QUANTISE_LAG)
             if step == len(v_pieces):
-                for g in range(M_PASSES):
-                    quantise_weights(v_grouped, v_words, v_scales, g)
+                quantise_weights("v")
             if step == len(weight_pieces):
-                quantise_weights(w_grouped, w_words, w_scales, 0)
+                quantise_weights("w")
             if 0 <= step - DIVIDE_LAG < TILES:
                 quantise_att(step - DIVIDE_LAG)
             if 0 <= step - PROJECT_LAG < TILES:

@@ -16,6 +16,7 @@ P = 128
 PACK = 4
 PAIR = 2
 K_PASS = P * PACK
+PSUM_BANKS = 8
 N_PIX = 4096
 M_POS = 1024
 DV = 512
@@ -48,9 +49,7 @@ def tile_selfattentionconv2d_pb_t_kernel(tc, q, k_pool, v_pool, imgs, w_out, gai
         codes = ctx.enter_context(tc.tile_pool(name="codes", bufs=ATTEND_LAG - QUANTISE_LAG + 2))
         by_group = ctx.enter_context(tc.tile_pool(name="by_group", bufs=2))
         stores = ctx.enter_context(tc.tile_pool(name="stores", bufs=4))
-        psum_s = ctx.enter_context(tc.psum_pool(name="psum_s", bufs=2 * M_PASSES))
-        psum_t = ctx.enter_context(tc.psum_pool(name="psum_t", bufs=2))
-        psum_o = ctx.enter_context(tc.psum_pool(name="psum_o", bufs=2))
+        psum = ctx.enter_context(tc.psum_pool(name="psum", bufs=PSUM_BANKS))
 
         q_sb = keep.tile([P, N_PIX], BF16)
         k_sb = keep.tile([P, M_POS], BF16)
@@ -96,7 +95,7 @@ def tile_selfattentionconv2d_pb_t_kernel(tc, q, k_pool, v_pool, imgs, w_out, gai
         weights_turned = {}
 
         def turn_weights(matrix, g, half):
-            turned = psum_o.tile([P, PAIR * PAIR, P], F32, tag="o")
+            turned = psum.tile([P, PAIR * PAIR, P], F32, tag="bank")
             for r in range(PAIR):
                 row_words = weights_sb[matrix][:, PAIR * half + r, :].bitcast(F32)
                 for u in range(PAIR):
@@ -135,7 +134,7 @@ def tile_selfattentionconv2d_pb_t_kernel(tc, q, k_pool, v_pool, imgs, w_out, gai
         y_banks = {}
 
         def scores(i):
-            s_banks[i] = [psum_s.tile([P, K_PASS], F32, name="s_ps") for g in range(M_PASSES)]
+            s_banks[i] = [psum.tile([P, K_PASS], F32, name="s_ps", tag="bank") for g in range(M_PASSES)]
             for g in range(M_PASSES):
                 nc.tensor.matmul(
                     out=s_banks[i][g][:],
@@ -150,7 +149,7 @@ def tile_selfattentionconv2d_pb_t_kernel(tc, q, k_pool, v_pool, imgs, w_out, gai
             for g in range(M_PASSES):
                 nc.vector.reduce_max(out=bank_max[:, g : g + 1], in_=s_banks[i][g][:], axis=AX.X)
             minus_max = small.tile([P, 1], F32)
-            nc.vector.tensor_scalar(
+            nc.gpsimd.tensor_scalar(
                 out=minus_max[:],
                 in0=bank_max[:, 0:1],
                 scalar1=bank_max[:, 1:2],
@@ -177,7 +176,7 @@ def tile_selfattentionconv2d_pb_t_kernel(tc, q, k_pool, v_pool, imgs, w_out, gai
             e_rows[i] = e_sb
 
         def turn_e(i):
-            turned = psum_t.tile([P, M_PASSES * PACK, P], BF16, tag="t")
+            turned = psum.tile([P, M_PASSES * PACK, P], BF16, tag="bank")
             for block in range(M_PASSES * PACK):
                 nc.tensor.transpose(turned[:, block, :], e_rows[i][:, block * P : (block + 1) * P], ident_bf[:])
             grouped = work.tile([P, M_PASSES, P, PACK], BF16, align_bytes=64, name="e_grouped")
@@ -196,10 +195,10 @@ def tile_selfattentionconv2d_pb_t_kernel(tc, q, k_pool, v_pool, imgs, w_out, gai
 
         def spread_inverse_sums(group):
             sums = small.tile([P, GROUP], F32)
-            nc.vector.reduce_sum(out=sums[:], in_=row_sums[group][:], axis=AX.X)
+            nc.gpsimd.tensor_tensor(out=sums[:], in0=row_sums[group][:, :, 0], in1=row_sums[group][:, :, 1], op=ALU.add)
             inverse = small.tile([P, GROUP], F32)
             nc.vector.reciprocal(out=inverse[:], in_=sums[:])
-            spread_ps = psum_t.tile([P, GROUP, P], F32, tag="t")
+            spread_ps = psum.tile([P, GROUP, P], F32, tag="bank")
             for j in range(GROUP):
                 nc.tensor.matmul(
                     out=spread_ps[:, j, :],
@@ -214,7 +213,7 @@ def tile_selfattentionconv2d_pb_t_kernel(tc, q, k_pool, v_pool, imgs, w_out, gai
 
         def attend(i):
             words, scales = e_packed[i]
-            att_ps = psum_o.tile([P, PACK, P], F32, tag="o")
+            att_ps = psum.tile([P, PACK, P], F32, tag="bank")
             for t in range(PACK):
                 for g in range(M_PASSES):
                     nc.tensor.matmul_mx(
@@ -255,7 +254,7 @@ def tile_selfattentionconv2d_pb_t_kernel(tc, q, k_pool, v_pool, imgs, w_out, gai
 
         def project(group, c):
             words, scales = att_packed[group]
-            y_ps = psum_o.tile([P, K_PASS], F32, tag="o")
+            y_ps = psum.tile([P, K_PASS], F32, tag="bank")
             nc.tensor.matmul_mx(
                 out=y_ps[:],
                 lhsT=weights_words["w"][:, 0, c * P : (c + 1) * P].bitcast(FP8X4),

@@ -29,12 +29,16 @@ CHUNKS = DV // P
 assert DV == K_PASS and C_OUT == DV and CHUNKS == GROUP == PACK
 assert M_PASSES == 2
 
+MAXIMUM_LAG = -1
+SCORES_LAG = -2
 TURN_LAG = 1
-QUANTISE_LAG = 3
-SUMS_LAG = 1
-ATTEND_LAG = GROUP + 1
-DIVIDE_LAG = ATTEND_LAG + 1
-PROJECT_LAG = DIVIDE_LAG + GROUP - 1
+QUANTISE_LAG = 2
+SUM_LAG = 1
+INVERT_LAG = 2
+ATTEND_LAG = 3
+TURN_ATT_LAG = 4
+QUANTISE_ATT_LAG = 5
+PROJECT_LAG = QUANTISE_ATT_LAG + PAIR
 FINISH_LAG = PROJECT_LAG + 1
 
 FLOPS = 2 * N_PIX * M_POS * P + 2 * N_PIX * M_POS * DV + 2 * N_PIX * DV * C_OUT
@@ -47,9 +51,12 @@ def tile_selfattentionconv2d_pb_t_kernel(tc, q, k_pool, v_pool, imgs, w_out, gai
         small = ctx.enter_context(tc.tile_pool(name="small", bufs=4))
         work = ctx.enter_context(tc.tile_pool(name="work", bufs=QUANTISE_LAG + 1))
         codes = ctx.enter_context(tc.tile_pool(name="codes", bufs=ATTEND_LAG - QUANTISE_LAG + 2))
-        by_group = ctx.enter_context(tc.tile_pool(name="by_group", bufs=2))
+        by_pair = ctx.enter_context(tc.tile_pool(name="by_pair", bufs=4))
         stores = ctx.enter_context(tc.tile_pool(name="stores", bufs=4))
-        psum = ctx.enter_context(tc.psum_pool(name="psum", bufs=PSUM_BANKS))
+        psum_s = ctx.enter_context(tc.psum_pool(name="psum_s", bufs=2 * M_PASSES))
+        psum_t = ctx.enter_context(tc.psum_pool(name="psum_t", bufs=2))
+        psum_a = ctx.enter_context(tc.psum_pool(name="psum_a", bufs=1))
+        psum_y = ctx.enter_context(tc.psum_pool(name="psum_y", bufs=1))
 
         q_sb = keep.tile([P, N_PIX], BF16)
         k_sb = keep.tile([P, M_POS], BF16)
@@ -65,9 +72,9 @@ def tile_selfattentionconv2d_pb_t_kernel(tc, q, k_pool, v_pool, imgs, w_out, gai
         nc.sync.dma_start(out=q_sb[:, 0:first], in_=q_view[:, 0:first])
         for g in range(M_PASSES):
             nc.sync.dma_start(out=k_sb[:, g * K_PASS : (g + 1) * K_PASS], in_=k_view[:, g * K_PASS : (g + 1) * K_PASS])
-        v_view = v_pool.rearrange("b (u p e) m -> p (b u) e m", u=PAIR, e=PAIR)
+        v_view = v_pool.rearrange("b (c p) m -> p (b c) m", p=P)
         for u in range(PAIR):
-            nc.sync.dma_start(out=v_sb[:, PAIR * u : PAIR * (u + 1), :], in_=v_view[:, u, :, :])
+            nc.sync.dma_start(out=v_sb[:, PAIR * u : PAIR * (u + 1), :], in_=v_view[:, PAIR * u : PAIR * (u + 1), :])
         nc.sync.dma_start(out=q_sb[:, first : N_PIX // 2], in_=q_view[:, first : N_PIX // 2])
         nc.sync.dma_start(out=w_sb[:], in_=w_out.rearrange("(c p) d -> p c d", p=P))
         nc.sync.dma_start(out=q_sb[:, N_PIX // 2 : N_PIX], in_=q_view[:, N_PIX // 2 : N_PIX])
@@ -75,8 +82,6 @@ def tile_selfattentionconv2d_pb_t_kernel(tc, q, k_pool, v_pool, imgs, w_out, gai
         for c in range(CHUNKS):
             nc.sync.dma_start(out=imgs_sb[:, c, :], in_=imgs_view[:, c, :])
 
-        ident_bf = keep.tile([P, P], BF16)
-        make_identity(nc, ident_bf[:])
         ident_f32 = keep.tile([P, P], F32)
         make_identity(nc, ident_f32[:])
         gain_f32 = keep.tile([P, 1], F32)
@@ -94,8 +99,8 @@ def tile_selfattentionconv2d_pb_t_kernel(tc, q, k_pool, v_pool, imgs, w_out, gai
             weights_scales[matrix] = keep.tile(shape, U8, align_bytes=64, name=matrix + "_scales")
         weights_turned = {}
 
-        def turn_weights(matrix, g, half):
-            turned = psum.tile([P, PAIR * PAIR, P], F32, tag="bank")
+        def turn_weights(matrix, g, half, pool):
+            turned = pool.tile([P, PAIR * PAIR, P], F32, tag="bank", name="turned")
             for r in range(PAIR):
                 row_words = weights_sb[matrix][:, PAIR * half + r, :].bitcast(F32)
                 for u in range(PAIR):
@@ -105,36 +110,41 @@ def tile_selfattentionconv2d_pb_t_kernel(tc, q, k_pool, v_pool, imgs, w_out, gai
                     )
             weights_turned[(matrix, g, half)] = turned
 
-        def group_weights(matrix, g, half):
+        def group_weights(matrix, g, half, engine):
             rows = slice(PAIR * half * P, PAIR * (half + 1) * P)
             grouped_words = weights_grouped[matrix][:, g, rows, :].rearrange("p n t -> p (n t)").bitcast(F32)
-            nc.vector.tensor_copy(
-                out=grouped_words.rearrange("p (r n u) -> p r n u", r=PAIR, u=PAIR),
-                in_=weights_turned[(matrix, g, half)][:].rearrange("p (r u) n -> p r n u", u=PAIR),
-            )
+            out_words = grouped_words.rearrange("p (r n u) -> p r n u", r=PAIR, u=PAIR)
+            in_words = weights_turned[(matrix, g, half)][:].rearrange("p (r u) n -> p r n u", u=PAIR)
+            if engine == "vector":
+                nc.vector.tensor_copy(out=out_words, in_=in_words)
+            else:
+                nc.scalar.copy(out=out_words, in_=in_words)
 
-        def quantise_weights(matrix):
-            for g in range(weights_passes[matrix]):
-                nc.vector.quantize_mx(
-                    out=weights_words[matrix][:, g, :].bitcast(FP8X4),
-                    scales=weights_scales[matrix][:, g, :],
-                    in_=weights_grouped[matrix][:, g, :, :].rearrange("p n t -> p (n t)"),
-                )
+        def quantise_weights(matrix, g):
+            nc.vector.quantize_mx(
+                out=weights_words[matrix][:, g, :].bitcast(FP8X4),
+                scales=weights_scales[matrix][:, g, :],
+                in_=weights_grouped[matrix][:, g, :, :].rearrange("p n t -> p (n t)"),
+            )
 
         s_banks = {}
         minus_maxima = {}
         e_rows = {}
+        e_turned = {}
         e_grouped = {}
         e_packed = {}
         row_sums = {}
+        sums_joined = {}
         inverse_sums = {}
         att_banks = {}
+        att_rows = {}
+        att_turned = {}
         att_grouped = {}
         att_packed = {}
         y_banks = {}
 
         def scores(i):
-            s_banks[i] = [psum.tile([P, K_PASS], F32, name="s_ps", tag="bank") for g in range(M_PASSES)]
+            s_banks[i] = [psum_s.tile([P, K_PASS], F32, name="s_ps", tag="bank") for g in range(M_PASSES)]
             for g in range(M_PASSES):
                 nc.tensor.matmul(
                     out=s_banks[i][g][:],
@@ -160,27 +170,34 @@ def tile_selfattentionconv2d_pb_t_kernel(tc, q, k_pool, v_pool, imgs, w_out, gai
             minus_maxima[i] = minus_max
 
         def exponentials(i):
-            group, j = divmod(i, GROUP)
+            pair, j = divmod(i, PAIR)
             if j == 0:
-                row_sums[group] = by_group.tile([P, GROUP, M_PASSES], F32, name="row_sums")
+                row_sums[pair] = by_pair.tile([P, PAIR, M_PASSES], F32, name="row_sums")
             e_sb = work.tile([P, M_POS], BF16)
             for g in range(M_PASSES):
                 nc.scalar.activation(
-                    out=e_sb[:, g * K_PASS : (g + 1) * K_PASS].rearrange("n (u e p) -> n u e p", u=PAIR, e=PAIR),
-                    in_=s_banks[i][g][:].rearrange("n (u p e) -> n u e p", u=PAIR, e=PAIR),
+                    out=e_sb[:, g * K_PASS : (g + 1) * K_PASS],
+                    in_=s_banks[i][g][:],
                     func=ACT.Exp,
                     bias=minus_maxima[i][:],
                     scale=1.0,
-                    accum_out=row_sums[group][:, j, g : g + 1],
+                    accum_out=row_sums[pair][:, j, g : g + 1],
                 )
             e_rows[i] = e_sb
 
         def turn_e(i):
-            turned = psum.tile([P, M_PASSES * PACK, P], BF16, tag="bank")
-            for block in range(M_PASSES * PACK):
-                nc.tensor.transpose(turned[:, block, :], e_rows[i][:, block * P : (block + 1) * P], ident_bf[:])
+            turned = psum_t.tile([P, M_PASSES * PAIR, P], F32, tag="bank")
+            row_words = e_rows[i][:].bitcast(F32)
+            for block in range(M_PASSES * PAIR):
+                nc.tensor.transpose(turned[:, block, :], row_words[:, block * P : (block + 1) * P], ident_f32[:])
+            e_turned[i] = turned
+
+        def copy_e(i):
             grouped = work.tile([P, M_PASSES, P, PACK], BF16, align_bytes=64, name="e_grouped")
-            nc.scalar.copy(out=grouped[:], in_=turned[:].rearrange("p (g t) n -> p g n t", t=PACK))
+            nc.scalar.copy(
+                out=grouped[:].rearrange("p g n t -> p (g n t)").bitcast(F32).rearrange("p (g n u) -> p g n u", g=M_PASSES, u=PAIR),
+                in_=e_turned[i][:].rearrange("p (g u) n -> p g n u", u=PAIR),
+            )
             e_grouped[i] = grouped
 
         def quantise_e(i):
@@ -193,123 +210,144 @@ def tile_selfattentionconv2d_pb_t_kernel(tc, q, k_pool, v_pool, imgs, w_out, gai
             )
             e_packed[i] = (words, scales)
 
-        def spread_inverse_sums(group):
-            sums = small.tile([P, GROUP], F32)
-            nc.gpsimd.tensor_tensor(out=sums[:], in0=row_sums[group][:, :, 0], in1=row_sums[group][:, :, 1], op=ALU.add)
-            inverse = small.tile([P, GROUP], F32)
-            nc.vector.reciprocal(out=inverse[:], in_=sums[:])
-            spread_ps = psum.tile([P, GROUP, P], F32, tag="bank")
-            for j in range(GROUP):
-                nc.tensor.matmul(
-                    out=spread_ps[:, j, :],
-                    lhsT=inverse[:, j : j + 1].to_broadcast([P, P]),
-                    rhs=ident_f32[:],
-                    start=True,
-                    stop=True,
-                )
-            spread = by_group.tile([P, GROUP, P], F32)
-            nc.scalar.copy(out=spread[:], in_=spread_ps[:])
-            inverse_sums[group] = spread
+        def join_sums(pair):
+            sums = small.tile([P, PAIR], F32)
+            nc.gpsimd.tensor_tensor(out=sums[:], in0=row_sums[pair][:, :, 0], in1=row_sums[pair][:, :, 1], op=ALU.add)
+            sums_joined[pair] = sums
 
-        def attend(i):
+        def invert_sums(pair):
+            inverse = by_pair.tile([P, PAIR], F32)
+            nc.vector.reciprocal(out=inverse[:], in_=sums_joined[pair][:])
+            inverse_sums[pair] = inverse
+
+        def attend(i, pool):
             words, scales = e_packed[i]
-            att_ps = psum.tile([P, PACK, P], F32, tag="bank")
-            for t in range(PACK):
-                for g in range(M_PASSES):
-                    nc.tensor.matmul_mx(
-                        out=att_ps[:, t, :],
-                        lhsT=weights_words["v"][:, g, t * P : (t + 1) * P].bitcast(FP8X4),
-                        lhsT_scale=weights_scales["v"][:, g, t * P : (t + 1) * P],
-                        rhs=words[:, g, :].bitcast(FP8X4),
-                        rhs_scale=scales[:, g, :],
-                        start=(g == 0),
-                        stop=(g == M_PASSES - 1),
-                    )
+            att_ps = pool.tile([P, DV], F32, tag="bank", name="att_ps")
+            for g in range(M_PASSES):
+                nc.tensor.matmul_mx(
+                    out=att_ps[:],
+                    lhsT=words[:, g, :].bitcast(FP8X4),
+                    lhsT_scale=scales[:, g, :],
+                    rhs=weights_words["v"][:, g, :].bitcast(FP8X4),
+                    rhs_scale=weights_scales["v"][:, g, :],
+                    start=(g == 0),
+                    stop=(g == M_PASSES - 1),
+                )
             att_banks[i] = att_ps
 
         def divide(i):
-            group, j = divmod(i, GROUP)
-            if j == 0:
-                att_grouped[group] = by_group.tile([P, GROUP, P, PACK], BF16, align_bytes=64, name="att_grouped")
-            nc.vector.tensor_tensor(
-                out=att_grouped[group][:, j, :, :],
-                in0=att_banks[i][:].rearrange("p t n -> p n t"),
-                in1=inverse_sums[group][:, j, :].unsqueeze(2).to_broadcast([P, P, PACK]),
-                op=ALU.mult,
-            )
+            pair, j = divmod(i, PAIR)
+            att = work.tile([P, DV], BF16, name="att_rows")
+            nc.scalar.activation(out=att[:], in_=att_banks[i][:], func=ACT.Copy, scale=inverse_sums[pair][:, j : j + 1])
+            att_rows[i] = att
 
-        def quantise_att(i):
-            group, j = divmod(i, GROUP)
-            if j == 0:
-                att_packed[group] = (
-                    by_group.tile([P, GROUP, P], U32, align_bytes=64, name="att_words"),
-                    by_group.tile([P, GROUP, P], U8, align_bytes=64, name="att_scales"),
-                )
-            words, scales = att_packed[group]
+        def turn_att(pair):
+            turned = psum_t.tile([P, PAIR * PAIR, P], F32, tag="bank")
+            for j in range(PAIR):
+                row_words = att_rows[PAIR * pair + j][:].bitcast(F32)
+                for u in range(PAIR):
+                    nc.tensor.transpose(turned[:, PAIR * j + u, :], row_words[:, u * P : (u + 1) * P], ident_f32[:])
+            att_turned[pair] = turned
+
+        def group_att(pair):
+            grouped = by_pair.tile([P, PAIR, P, PACK], BF16, align_bytes=64, name="att_grouped")
+            out_words = grouped[:].rearrange("p j n t -> p (j n t)").bitcast(F32).rearrange("p (j n u) -> p j n u", j=PAIR, u=PAIR)
+            in_words = att_turned[pair][:].rearrange("p (j u) n -> p j n u", u=PAIR)
+            if pair % 2 == 0:
+                nc.vector.tensor_copy(out=out_words, in_=in_words)
+            else:
+                nc.scalar.copy(out=out_words, in_=in_words)
+            att_grouped[pair] = grouped
+
+        def quantise_att(pair):
+            words = by_pair.tile([P, PAIR * P], U32, align_bytes=64, name="att_words")
+            scales = by_pair.tile([P, PAIR * P], U8, align_bytes=64, name="att_scales")
             nc.vector.quantize_mx(
-                out=words[:, j, :].bitcast(FP8X4),
-                scales=scales[:, j, :],
-                in_=att_grouped[group][:, j, :, :].rearrange("p n t -> p (n t)"),
+                out=words[:].bitcast(FP8X4),
+                scales=scales[:],
+                in_=att_grouped[pair][:].rearrange("p j n t -> p (j n t)"),
             )
+            att_packed[pair] = (words, scales)
 
-        def project(group, c):
-            words, scales = att_packed[group]
-            y_ps = psum.tile([P, K_PASS], F32, tag="bank")
-            nc.tensor.matmul_mx(
-                out=y_ps[:],
-                lhsT=weights_words["w"][:, 0, c * P : (c + 1) * P].bitcast(FP8X4),
-                lhsT_scale=weights_scales["w"][:, 0, c * P : (c + 1) * P],
-                rhs=words[:].rearrange("p j n -> p (j n)").bitcast(FP8X4),
-                rhs_scale=scales[:].rearrange("p j n -> p (j n)"),
-                start=True,
-                stop=True,
-            )
-            y_banks[(group, c)] = y_ps
+        def project(pair, half, pool):
+            words, scales = att_packed[pair]
+            y_ps = pool.tile([P, PAIR, PAIR * P], F32, tag="bank", name="y_ps")
+            for r in range(PAIR):
+                c = PAIR * half + r
+                nc.tensor.matmul_mx(
+                    out=y_ps[:, r, :],
+                    lhsT=weights_words["w"][:, 0, c * P : (c + 1) * P].bitcast(FP8X4),
+                    lhsT_scale=weights_scales["w"][:, 0, c * P : (c + 1) * P],
+                    rhs=words[:].bitcast(FP8X4),
+                    rhs_scale=scales[:],
+                    start=True,
+                    stop=True,
+                )
+            y_banks[(pair, half)] = y_ps
 
-        def finish(group, c):
-            cols = slice(group * GROUP * P, (group + 1) * GROUP * P)
-            result = stores.tile([P, GROUP * P], F32)
+        def finish(pair, half):
+            chunks = slice(PAIR * half, PAIR * (half + 1))
+            cols = slice(pair * PAIR * P, (pair + 1) * PAIR * P)
+            result = stores.tile([P, PAIR, PAIR * P], F32)
             nc.vector.scalar_tensor_tensor(
                 out=result[:],
-                in0=y_banks[(group, c)][:],
+                in0=y_banks[(pair, half)][:],
                 scalar=gain_f32[:, 0:1],
-                in1=imgs_sb[:, c, cols],
+                in1=imgs_sb[:, chunks, cols],
                 op0=ALU.mult,
                 op1=ALU.add,
             )
-            nc.sync.dma_start(out=out_view[:, c, cols], in_=result[:])
+            nc.sync.dma_start(out=out_view[:, chunks, cols], in_=result[:])
 
-        v_pieces = [("v", g, half) for g in range(M_PASSES) for half in range(CHUNKS // PAIR)]
-        w_pieces = [("w", 0, half) for half in range(CHUNKS // PAIR)]
-        weight_pieces = v_pieces + w_pieces
-        scores(0)
-        for step in range(TILES + FINISH_LAG):
-            if step < TILES:
-                row_maximum(step)
-                exponentials(step)
-            if step + 1 < TILES:
-                scores(step + 1)
-            if 0 <= step - TURN_LAG < TILES:
-                turn_e(step - TURN_LAG)
-            if 0 <= step - 1 < len(weight_pieces):
-                group_weights(*weight_pieces[step - 1])
-            if step < len(weight_pieces):
-                turn_weights(*weight_pieces[step])
-            if 0 <= step - DIVIDE_LAG < TILES:
-                divide(step - DIVIDE_LAG)
-            if 0 <= step - ATTEND_LAG < TILES:
-                attend(step - ATTEND_LAG)
-            if step >= FINISH_LAG:
-                finish(*divmod(step - FINISH_LAG, CHUNKS))
-            if 0 <= step - QUANTISE_LAG < TILES:
-                quantise_e(step - QUANTISE_LAG)
-            if step == len(v_pieces):
-                quantise_weights("v")
-            if step == len(weight_pieces):
-                quantise_weights("w")
-            if 0 <= step - DIVIDE_LAG < TILES:
-                quantise_att(step - DIVIDE_LAG)
-            if 0 <= step - PROJECT_LAG < TILES:
-                project(*divmod(step - PROJECT_LAG, CHUNKS))
-            if 0 <= step - SUMS_LAG < TILES and (step - SUMS_LAG) % GROUP == GROUP - 1:
-                spread_inverse_sums((step - SUMS_LAG) // GROUP)
+        weight_pieces = {
+            0: [("v", 0, 0, psum_a, "vector")],
+            1: [("v", 1, 0, psum_y, "scalar"), ("v", 0, 1, psum_a, "vector")],
+            2: [("v", 1, 1, psum_y, "scalar")],
+            3: [("w", 0, 0, psum_y, "vector")],
+            4: [("w", 0, 1, psum_y, "scalar")],
+        }
+        weight_quants = {2: [("v", 0)], 3: [("v", 1)], 5: [("w", 0)]}
+
+        def tile_of(step, lag):
+            return [step - lag] if 0 <= step - lag < TILES else []
+
+        def pair_of(step, lag):
+            return [i // PAIR for i in tile_of(step, lag) if i % PAIR == PAIR - 1]
+
+        with tc.manual_schedule():
+            for step in range(SCORES_LAG, TILES + FINISH_LAG):
+                for matrix, g in weight_quants.get(step, []):
+                    quantise_weights(matrix, g)
+                for i in tile_of(step, FINISH_LAG):
+                    finish(*divmod(i, PAIR))
+                for i in tile_of(step, TURN_LAG):
+                    turn_e(i)
+                for pair in pair_of(step, TURN_ATT_LAG):
+                    turn_att(pair)
+                for i in tile_of(step, 0):
+                    exponentials(i)
+                for i in tile_of(step, MAXIMUM_LAG):
+                    row_maximum(i)
+                for pair in pair_of(step, INVERT_LAG):
+                    invert_sums(pair)
+                for i in tile_of(step, ATTEND_LAG):
+                    attend(i, psum_a if step < TILES else psum_s)
+                for i in tile_of(step, PROJECT_LAG):
+                    project(*divmod(i, PAIR), psum_y if step < TILES else psum_s)
+                for i in tile_of(step, SCORES_LAG):
+                    scores(i)
+                for i in tile_of(step, TURN_LAG):
+                    copy_e(i)
+                for i in tile_of(step, ATTEND_LAG):
+                    divide(i)
+                for i in tile_of(step, QUANTISE_LAG):
+                    quantise_e(i)
+                for matrix, g, half, pool, engine in weight_pieces.get(step, []):
+                    turn_weights(matrix, g, half, pool)
+                    group_weights(matrix, g, half, engine)
+                for pair in pair_of(step, TURN_ATT_LAG):
+                    group_att(pair)
+                for pair in pair_of(step, QUANTISE_ATT_LAG):
+                    quantise_att(pair)
+                for pair in pair_of(step, SUM_LAG):
+                    join_sums(pair)

@@ -52,11 +52,8 @@ def tile_selfattentionconv2d_pb_t_kernel(tc, q, k_pool, v_pool, imgs, w_out, gai
         work = ctx.enter_context(tc.tile_pool(name="work", bufs=QUANTISE_LAG + 1))
         codes = ctx.enter_context(tc.tile_pool(name="codes", bufs=ATTEND_LAG - QUANTISE_LAG + 2))
         by_pair = ctx.enter_context(tc.tile_pool(name="by_pair", bufs=4))
-        stores = ctx.enter_context(tc.tile_pool(name="stores", bufs=4))
-        psum_s = ctx.enter_context(tc.psum_pool(name="psum_s", bufs=2 * M_PASSES))
-        psum_t = ctx.enter_context(tc.psum_pool(name="psum_t", bufs=2))
-        psum_a = ctx.enter_context(tc.psum_pool(name="psum_a", bufs=1))
-        psum_y = ctx.enter_context(tc.psum_pool(name="psum_y", bufs=1))
+        stores = ctx.enter_context(tc.tile_pool(name="stores", bufs=8))
+        psum = ctx.enter_context(tc.psum_pool(name="psum", bufs=PSUM_BANKS))
 
         q_sb = keep.tile([P, N_PIX], BF16)
         k_sb = keep.tile([P, M_POS], BF16)
@@ -99,8 +96,8 @@ def tile_selfattentionconv2d_pb_t_kernel(tc, q, k_pool, v_pool, imgs, w_out, gai
             weights_scales[matrix] = keep.tile(shape, U8, align_bytes=64, name=matrix + "_scales")
         weights_turned = {}
 
-        def turn_weights(matrix, g, half, pool):
-            turned = pool.tile([P, PAIR * PAIR, P], F32, tag="bank", name="turned")
+        def turn_weights(matrix, g, half):
+            turned = psum.tile([P, PAIR * PAIR, P], F32, tag="bank", name="turned")
             for r in range(PAIR):
                 row_words = weights_sb[matrix][:, PAIR * half + r, :].bitcast(F32)
                 for u in range(PAIR):
@@ -110,12 +107,12 @@ def tile_selfattentionconv2d_pb_t_kernel(tc, q, k_pool, v_pool, imgs, w_out, gai
                     )
             weights_turned[(matrix, g, half)] = turned
 
-        def group_weights(matrix, g, half, engine):
+        def group_weights(matrix, g, half):
             rows = slice(PAIR * half * P, PAIR * (half + 1) * P)
             grouped_words = weights_grouped[matrix][:, g, rows, :].rearrange("p n t -> p (n t)").bitcast(F32)
             out_words = grouped_words.rearrange("p (r n u) -> p r n u", r=PAIR, u=PAIR)
             in_words = weights_turned[(matrix, g, half)][:].rearrange("p (r u) n -> p r n u", u=PAIR)
-            if engine == "vector":
+            if g == 0:
                 nc.vector.tensor_copy(out=out_words, in_=in_words)
             else:
                 nc.scalar.copy(out=out_words, in_=in_words)
@@ -144,7 +141,7 @@ def tile_selfattentionconv2d_pb_t_kernel(tc, q, k_pool, v_pool, imgs, w_out, gai
         y_banks = {}
 
         def scores(i):
-            s_banks[i] = [psum_s.tile([P, K_PASS], F32, name="s_ps", tag="bank") for g in range(M_PASSES)]
+            s_banks[i] = [psum.tile([P, K_PASS], F32, name="s_ps", tag="bank") for g in range(M_PASSES)]
             for g in range(M_PASSES):
                 nc.tensor.matmul(
                     out=s_banks[i][g][:],
@@ -186,7 +183,7 @@ def tile_selfattentionconv2d_pb_t_kernel(tc, q, k_pool, v_pool, imgs, w_out, gai
             e_rows[i] = e_sb
 
         def turn_e(i):
-            turned = psum_t.tile([P, M_PASSES * PAIR, P], F32, tag="bank")
+            turned = psum.tile([P, M_PASSES * PAIR, P], F32, tag="bank")
             row_words = e_rows[i][:].bitcast(F32)
             for block in range(M_PASSES * PAIR):
                 nc.tensor.transpose(turned[:, block, :], row_words[:, block * P : (block + 1) * P], ident_f32[:])
@@ -220,9 +217,9 @@ def tile_selfattentionconv2d_pb_t_kernel(tc, q, k_pool, v_pool, imgs, w_out, gai
             nc.vector.reciprocal(out=inverse[:], in_=sums_joined[pair][:])
             inverse_sums[pair] = inverse
 
-        def attend(i, pool):
+        def attend(i):
             words, scales = e_packed[i]
-            att_ps = pool.tile([P, DV], F32, tag="bank", name="att_ps")
+            att_ps = psum.tile([P, DV], F32, tag="bank", name="att_ps")
             for g in range(M_PASSES):
                 nc.tensor.matmul_mx(
                     out=att_ps[:],
@@ -241,23 +238,25 @@ def tile_selfattentionconv2d_pb_t_kernel(tc, q, k_pool, v_pool, imgs, w_out, gai
             nc.scalar.activation(out=att[:], in_=att_banks[i][:], func=ACT.Copy, scale=inverse_sums[pair][:, j : j + 1])
             att_rows[i] = att
 
-        def turn_att(pair):
-            turned = psum_t.tile([P, PAIR * PAIR, P], F32, tag="bank")
-            for j in range(PAIR):
-                row_words = att_rows[PAIR * pair + j][:].bitcast(F32)
+        def turn_att(tiles):
+            turned = psum.tile([P, PAIR * len(tiles), P], F32, tag="bank", name="att_turned")
+            for j, i in enumerate(tiles):
+                row_words = att_rows[i][:].bitcast(F32)
                 for u in range(PAIR):
                     nc.tensor.transpose(turned[:, PAIR * j + u, :], row_words[:, u * P : (u + 1) * P], ident_f32[:])
-            att_turned[pair] = turned
+            att_turned[tiles[0]] = turned
 
-        def group_att(pair):
-            grouped = by_pair.tile([P, PAIR, P, PACK], BF16, align_bytes=64, name="att_grouped")
-            out_words = grouped[:].rearrange("p j n t -> p (j n t)").bitcast(F32).rearrange("p (j n u) -> p j n u", j=PAIR, u=PAIR)
-            in_words = att_turned[pair][:].rearrange("p (j u) n -> p j n u", u=PAIR)
-            if pair % 2 == 0:
+        def group_att(tiles, engine):
+            pair, j = divmod(tiles[0], PAIR)
+            if j == 0:
+                att_grouped[pair] = by_pair.tile([P, PAIR, P, PACK], BF16, align_bytes=64, name="att_grouped")
+            grouped = att_grouped[pair][:, j : j + len(tiles), :, :].rearrange("p j n t -> p (j n t)").bitcast(F32)
+            out_words = grouped.rearrange("p (j n u) -> p j n u", j=len(tiles), u=PAIR)
+            in_words = att_turned[tiles[0]][:].rearrange("p (j u) n -> p j n u", u=PAIR)
+            if engine == "vector":
                 nc.vector.tensor_copy(out=out_words, in_=in_words)
             else:
                 nc.scalar.copy(out=out_words, in_=in_words)
-            att_grouped[pair] = grouped
 
         def quantise_att(pair):
             words = by_pair.tile([P, PAIR * P], U32, align_bytes=64, name="att_words")
@@ -269,9 +268,9 @@ def tile_selfattentionconv2d_pb_t_kernel(tc, q, k_pool, v_pool, imgs, w_out, gai
             )
             att_packed[pair] = (words, scales)
 
-        def project(pair, half, pool):
+        def project(pair, half):
             words, scales = att_packed[pair]
-            y_ps = pool.tile([P, PAIR, PAIR * P], F32, tag="bank", name="y_ps")
+            y_ps = psum.tile([P, PAIR, PAIR * P], F32, tag="bank", name="y_ps")
             for r in range(PAIR):
                 c = PAIR * half + r
                 nc.tensor.matmul_mx(
@@ -299,14 +298,7 @@ def tile_selfattentionconv2d_pb_t_kernel(tc, q, k_pool, v_pool, imgs, w_out, gai
             )
             nc.sync.dma_start(out=out_view[:, chunks, cols], in_=result[:])
 
-        weight_pieces = {
-            0: [("v", 0, 0, psum_a, "vector")],
-            1: [("v", 1, 0, psum_y, "scalar"), ("v", 0, 1, psum_a, "vector")],
-            2: [("v", 1, 1, psum_y, "scalar")],
-            3: [("w", 0, 0, psum_y, "vector")],
-            4: [("w", 0, 1, psum_y, "scalar")],
-        }
-        weight_quants = {2: [("v", 0)], 3: [("v", 1)], 5: [("w", 0)]}
+        weight_steps = [[("v", 0, 0), ("v", 1, 0)], [("v", 0, 1), ("v", 1, 1)], [("w", 0, 0)], [("w", 0, 1)]]
 
         def tile_of(step, lag):
             return [step - lag] if 0 <= step - lag < TILES else []
@@ -315,15 +307,16 @@ def tile_selfattentionconv2d_pb_t_kernel(tc, q, k_pool, v_pool, imgs, w_out, gai
             return [i // PAIR for i in tile_of(step, lag) if i % PAIR == PAIR - 1]
 
         with tc.manual_schedule():
-            for step in range(SCORES_LAG, TILES + FINISH_LAG):
-                for matrix, g in weight_quants.get(step, []):
-                    quantise_weights(matrix, g)
-                for i in tile_of(step, FINISH_LAG):
-                    finish(*divmod(i, PAIR))
+            for step in range(SCORES_LAG, TILES):
+                if step == 2:
+                    quantise_weights("v", 0)
+                    quantise_weights("v", 1)
+                if step == len(weight_steps):
+                    quantise_weights("w", 0)
                 for i in tile_of(step, TURN_LAG):
                     turn_e(i)
                 for pair in pair_of(step, TURN_ATT_LAG):
-                    turn_att(pair)
+                    turn_att([PAIR * pair, PAIR * pair + 1])
                 for i in tile_of(step, 0):
                     exponentials(i)
                 for i in tile_of(step, MAXIMUM_LAG):
@@ -331,9 +324,9 @@ def tile_selfattentionconv2d_pb_t_kernel(tc, q, k_pool, v_pool, imgs, w_out, gai
                 for pair in pair_of(step, INVERT_LAG):
                     invert_sums(pair)
                 for i in tile_of(step, ATTEND_LAG):
-                    attend(i, psum_a if step < TILES else psum_s)
+                    attend(i)
                 for i in tile_of(step, PROJECT_LAG):
-                    project(*divmod(i, PAIR), psum_y if step < TILES else psum_s)
+                    project(*divmod(i, PAIR))
                 for i in tile_of(step, SCORES_LAG):
                     scores(i)
                 for i in tile_of(step, TURN_LAG):
@@ -342,12 +335,50 @@ def tile_selfattentionconv2d_pb_t_kernel(tc, q, k_pool, v_pool, imgs, w_out, gai
                     divide(i)
                 for i in tile_of(step, QUANTISE_LAG):
                     quantise_e(i)
-                for matrix, g, half, pool, engine in weight_pieces.get(step, []):
-                    turn_weights(matrix, g, half, pool)
-                    group_weights(matrix, g, half, engine)
+                for i in tile_of(step, FINISH_LAG):
+                    finish(*divmod(i, PAIR))
+                for matrix, g, half in weight_steps[step] if 0 <= step < len(weight_steps) else []:
+                    turn_weights(matrix, g, half)
+                    group_weights(matrix, g, half)
                 for pair in pair_of(step, TURN_ATT_LAG):
-                    group_att(pair)
+                    group_att([PAIR * pair, PAIR * pair + 1], "scalar" if pair % 3 == 1 and pair < 13 else "vector")
                 for pair in pair_of(step, QUANTISE_ATT_LAG):
                     quantise_att(pair)
                 for pair in pair_of(step, SUM_LAG):
                     join_sums(pair)
+            join_sums(15)
+            attend(29)
+            turn_e(31)
+            copy_e(31)
+            divide(29)
+            project(12,1)
+            finish(12,0)
+            quantise_e(30)
+            quantise_att(13)
+            finish(12,1)
+            invert_sums(15)
+            quantise_e(31)
+            attend(30)
+            divide(30)
+            turn_att([28,29])
+            group_att([28,29],"vector")
+            project(13,0)
+            attend(31)
+            divide(31)
+            quantise_att(14)
+            finish(13,0)
+            turn_att([30])
+            group_att([30],"scalar")
+            project(13,1)
+            project(14,0)
+            finish(13,1)
+            turn_att([31])
+            group_att([31],"scalar")
+            project(14,1)
+            finish(14,0)
+            quantise_att(15)
+            finish(14,1)
+            project(15,0)
+            project(15,1)
+            finish(15,0)
+            finish(15,1)

@@ -75,14 +75,12 @@ def tile_selfattentionconv2d_pb_t_kernel(tc, q, k_pool, v_pool, imgs, w_out, gai
         nc.sync.dma_start(out=q_sb[:, first : N_PIX // 2], in_=q_view[:, first : N_PIX // 2])
         nc.sync.dma_start(out=w_sb[:], in_=w_out.rearrange("(c p) d -> p c d", p=P))
         nc.sync.dma_start(out=q_sb[:, N_PIX // 2 : N_PIX], in_=q_view[:, N_PIX // 2 : N_PIX])
-        nc.scalar.dma_start(out=gain_bf[:], in_=gain.partition_broadcast(P))
         for c in range(CHUNKS):
             nc.sync.dma_start(out=imgs_sb[:, c, :], in_=imgs_view[:, c, :])
+        nc.sync.dma_start(out=gain_bf[:], in_=gain.partition_broadcast(P))
 
         ident_f32 = keep.tile([P, P], F32)
         make_identity(nc, ident_f32[:])
-        gain_f32 = keep.tile([P, 1], F32)
-        nc.vector.tensor_copy(out=gain_f32[:], in_=gain_bf[:])
 
         weights_sb = {"v": v_sb, "w": w_sb}
         weights_passes = {"v": M_PASSES, "w": 1}
@@ -156,7 +154,7 @@ def tile_selfattentionconv2d_pb_t_kernel(tc, q, k_pool, v_pool, imgs, w_out, gai
             for g in range(M_PASSES):
                 nc.vector.reduce_max(out=bank_max[:, g : g + 1], in_=s_banks[i][g][:], axis=AX.X)
             minus_max = small.tile([P, 1], F32)
-            nc.gpsimd.tensor_scalar(
+            (nc.vector if i == 0 else nc.gpsimd).tensor_scalar(
                 out=minus_max[:],
                 in0=bank_max[:, 0:1],
                 scalar1=bank_max[:, 1:2],
@@ -291,7 +289,7 @@ def tile_selfattentionconv2d_pb_t_kernel(tc, q, k_pool, v_pool, imgs, w_out, gai
             nc.vector.scalar_tensor_tensor(
                 out=result[:],
                 in0=y_banks[(pair, half)][:],
-                scalar=gain_f32[:, 0:1],
+                scalar=gain_bf[:, 0:1],
                 in1=imgs_sb[:, chunks, cols],
                 op0=ALU.mult,
                 op1=ALU.add,

@@ -34,7 +34,7 @@ SCORES_LAG = -2
 TURN_LAG = 1
 QUANTISE_LAG = 2
 SUM_LAG = 1
-INVERT_LAG = 2
+INVERT_LAG = 1
 ATTEND_LAG = 3
 TURN_ATT_LAG = 4
 QUANTISE_ATT_LAG = 5
@@ -81,6 +81,9 @@ def tile_selfattentionconv2d_pb_t_kernel(tc, q, k_pool, v_pool, imgs, w_out, gai
 
         ident_f32 = keep.tile([P, P], F32)
         make_identity(nc, ident_f32[:])
+
+        minus_one = keep.tile([P, PAIR], F32)
+        nc.gpsimd.memset(minus_one[:], -1.0)
 
         weights_sb = {"v": v_sb, "w": w_sb}
         weights_passes = {"v": M_PASSES, "w": 1}
@@ -180,30 +183,36 @@ def tile_selfattentionconv2d_pb_t_kernel(tc, q, k_pool, v_pool, imgs, w_out, gai
                 )
             e_rows[i] = e_sb
 
-        def turn_e(i):
-            turned = psum.tile([P, M_PASSES * PAIR, P], F32, tag="bank")
+        def turn_e(i, passes):
+            turned = psum.tile([P, PAIR * len(passes), P], F32, tag="bank", name="e_turned")
             row_words = e_rows[i][:].bitcast(F32)
-            for block in range(M_PASSES * PAIR):
-                nc.tensor.transpose(turned[:, block, :], row_words[:, block * P : (block + 1) * P], ident_f32[:])
-            e_turned[i] = turned
+            for n in range(PAIR * len(passes)):
+                block = PAIR * passes[0] + n
+                nc.tensor.transpose(turned[:, n, :], row_words[:, block * P : (block + 1) * P], ident_f32[:])
+            e_turned[(i, passes[0])] = turned
 
-        def copy_e(i):
-            grouped = work.tile([P, M_PASSES, P, PACK], BF16, align_bytes=64, name="e_grouped")
-            nc.scalar.copy(
-                out=grouped[:].rearrange("p g n t -> p (g n t)").bitcast(F32).rearrange("p (g n u) -> p g n u", g=M_PASSES, u=PAIR),
-                in_=e_turned[i][:].rearrange("p (g u) n -> p g n u", u=PAIR),
+        def copy_e(i, passes, engine):
+            if passes[0] == 0:
+                e_grouped[i] = work.tile([P, M_PASSES, P, PACK], BF16, align_bytes=64, name="e_grouped")
+            grouped = e_grouped[i][:, passes[0] : passes[-1] + 1, :, :].rearrange("p g n t -> p (g n t)").bitcast(F32)
+            engine(
+                out=grouped.rearrange("p (g n u) -> p g n u", g=len(passes), u=PAIR),
+                in_=e_turned[(i, passes[0])][:].rearrange("p (g u) n -> p g n u", u=PAIR),
             )
-            e_grouped[i] = grouped
 
-        def quantise_e(i):
-            words = codes.tile([P, M_PASSES, P], U32, align_bytes=64, name="e_words")
-            scales = codes.tile([P, M_PASSES, P], U8, align_bytes=64, name="e_scales")
+        def quantise_e(i, passes):
+            if passes[0] == 0:
+                e_packed[i] = (
+                    codes.tile([P, M_PASSES, P], U32, align_bytes=64, name="e_words"),
+                    codes.tile([P, M_PASSES, P], U8, align_bytes=64, name="e_scales"),
+                )
+            words, scales = e_packed[i]
+            span = slice(passes[0], passes[-1] + 1)
             nc.vector.quantize_mx(
-                out=words[:].rearrange("p g n -> p (g n)").bitcast(FP8X4),
-                scales=scales[:].rearrange("p g n -> p (g n)"),
-                in_=e_grouped[i][:].rearrange("p g n t -> p (g n t)"),
+                out=words[:, span, :].rearrange("p g n -> p (g n)").bitcast(FP8X4),
+                scales=scales[:, span, :].rearrange("p g n -> p (g n)"),
+                in_=e_grouped[i][:, span, :, :].rearrange("p g n t -> p (g n t)"),
             )
-            e_packed[i] = (words, scales)
 
         def join_sums(pair):
             sums = small.tile([P, PAIR], F32)
@@ -212,7 +221,7 @@ def tile_selfattentionconv2d_pb_t_kernel(tc, q, k_pool, v_pool, imgs, w_out, gai
 
         def invert_sums(pair):
             inverse = by_pair.tile([P, PAIR], F32)
-            nc.vector.reciprocal(out=inverse[:], in_=sums_joined[pair][:])
+            nc.gpsimd.tensor_tensor(out=inverse[:], in0=sums_joined[pair][:], in1=minus_one[:], op=ALU.pow)
             inverse_sums[pair] = inverse
 
         def attend(i):
@@ -251,132 +260,157 @@ def tile_selfattentionconv2d_pb_t_kernel(tc, q, k_pool, v_pool, imgs, w_out, gai
             grouped = att_grouped[pair][:, j : j + len(tiles), :, :].rearrange("p j n t -> p (j n t)").bitcast(F32)
             out_words = grouped.rearrange("p (j n u) -> p j n u", j=len(tiles), u=PAIR)
             in_words = att_turned[tiles[0]][:].rearrange("p (j u) n -> p j n u", u=PAIR)
-            if engine == "vector":
-                nc.vector.tensor_copy(out=out_words, in_=in_words)
-            else:
-                nc.scalar.copy(out=out_words, in_=in_words)
+            engine(out=out_words, in_=in_words)
 
-        def quantise_att(pair):
-            words = by_pair.tile([P, PAIR * P], U32, align_bytes=64, name="att_words")
-            scales = by_pair.tile([P, PAIR * P], U8, align_bytes=64, name="att_scales")
-            nc.vector.quantize_mx(
-                out=words[:].bitcast(FP8X4),
-                scales=scales[:],
-                in_=att_grouped[pair][:].rearrange("p j n t -> p (j n t)"),
-            )
-            att_packed[pair] = (words, scales)
-
-        def project(pair, half):
+        def quantise_att(tiles):
+            pair, j = divmod(tiles[0], PAIR)
+            if j == 0:
+                att_packed[pair] = (
+                    by_pair.tile([P, PAIR, P], U32, align_bytes=64, name="att_words"),
+                    by_pair.tile([P, PAIR, P], U8, align_bytes=64, name="att_scales"),
+                )
             words, scales = att_packed[pair]
-            y_ps = psum.tile([P, PAIR, PAIR * P], F32, tag="bank", name="y_ps")
-            for r in range(PAIR):
-                c = PAIR * half + r
+            span = slice(j, j + len(tiles))
+            nc.vector.quantize_mx(
+                out=words[:, span, :].rearrange("p j n -> p (j n)").bitcast(FP8X4),
+                scales=scales[:, span, :].rearrange("p j n -> p (j n)"),
+                in_=att_grouped[pair][:, span, :, :].rearrange("p j n t -> p (j n t)"),
+            )
+
+        def project(tiles, chunks):
+            pair, j = divmod(tiles[0], PAIR)
+            words, scales = att_packed[pair]
+            span = slice(j, j + len(tiles))
+            y_ps = psum.tile([P, len(chunks), len(tiles) * P], F32, tag="bank", name="y_ps")
+            for n, c in enumerate(chunks):
                 nc.tensor.matmul_mx(
-                    out=y_ps[:, r, :],
+                    out=y_ps[:, n, :],
                     lhsT=weights_words["w"][:, 0, c * P : (c + 1) * P].bitcast(FP8X4),
                     lhsT_scale=weights_scales["w"][:, 0, c * P : (c + 1) * P],
-                    rhs=words[:].bitcast(FP8X4),
-                    rhs_scale=scales[:],
+                    rhs=words[:, span, :].rearrange("p j n -> p (j n)").bitcast(FP8X4),
+                    rhs_scale=scales[:, span, :].rearrange("p j n -> p (j n)"),
                     start=True,
                     stop=True,
                 )
-            y_banks[(pair, half)] = y_ps
+            y_banks[(tiles[0], chunks[0])] = y_ps
 
-        def finish(pair, half):
-            chunks = slice(PAIR * half, PAIR * (half + 1))
-            cols = slice(pair * PAIR * P, (pair + 1) * PAIR * P)
-            result = stores.tile([P, PAIR, PAIR * P], F32)
+        def finish(tiles, chunks):
+            span = slice(chunks[0], chunks[-1] + 1)
+            cols = slice(tiles[0] * P, (tiles[-1] + 1) * P)
+            result = stores.tile([P, len(chunks), len(tiles) * P], F32)
             nc.vector.scalar_tensor_tensor(
                 out=result[:],
-                in0=y_banks[(pair, half)][:],
+                in0=y_banks[(tiles[0], chunks[0])][:],
                 scalar=gain_bf[:, 0:1],
-                in1=imgs_sb[:, chunks, cols],
+                in1=imgs_sb[:, span, cols],
                 op0=ALU.mult,
                 op1=ALU.add,
             )
-            nc.sync.dma_start(out=out_view[:, chunks, cols], in_=result[:])
+            nc.sync.dma_start(out=out_view[:, span, cols], in_=result[:])
 
-        weight_steps = [[("v", 0, 0), ("v", 1, 0)], [("v", 0, 1), ("v", 1, 1)], [("w", 0, 0)], [("w", 0, 1)]]
+        weight_steps = {0: [("v", 0, 0), ("v", 1, 0)], 1: [("v", 0, 1), ("v", 1, 1)], 2: [("w", 0, 0)], 3: [("w", 0, 1)]}
+
+        BOTH = [0, 1]
+        vector_copy = nc.vector.tensor_copy
+        scalar_copy = nc.scalar.copy
 
         def tile_of(step, lag):
             return [step - lag] if 0 <= step - lag < TILES else []
 
         def pair_of(step, lag):
-            return [i // PAIR for i in tile_of(step, lag) if i % PAIR == PAIR - 1]
+            return [[i - 1, i] for i in tile_of(step, lag) if i % PAIR == PAIR - 1]
+
+        def pair_and_half(i):
+            pair, half = divmod(i, PAIR)
+            return [PAIR * pair, PAIR * pair + 1], [PAIR * half, PAIR * half + 1]
 
         with tc.manual_schedule():
-            for step in range(SCORES_LAG, TILES):
-                if step == 2:
-                    quantise_weights("v", 0)
-                    quantise_weights("v", 1)
-                if step == len(weight_steps):
-                    quantise_weights("w", 0)
+            for step in range(SCORES_LAG, TILES - 1):
+                for tiles in pair_of(step, SUM_LAG):
+                    join_sums(tiles[0] // PAIR)
+                for tiles in pair_of(step, INVERT_LAG):
+                    invert_sums(tiles[0] // PAIR)
                 for i in tile_of(step, TURN_LAG):
-                    turn_e(i)
-                for pair in pair_of(step, TURN_ATT_LAG):
-                    turn_att([PAIR * pair, PAIR * pair + 1])
+                    turn_e(i, BOTH)
+                for tiles in pair_of(step, TURN_ATT_LAG):
+                    turn_att(tiles)
                 for i in tile_of(step, 0):
                     exponentials(i)
                 for i in tile_of(step, MAXIMUM_LAG):
                     row_maximum(i)
-                for pair in pair_of(step, INVERT_LAG):
-                    invert_sums(pair)
+                if step == 2:
+                    quantise_weights("v", 0)
+                    quantise_weights("v", 1)
+                if step == 4:
+                    quantise_weights("w", 0)
                 for i in tile_of(step, ATTEND_LAG):
                     attend(i)
                 for i in tile_of(step, PROJECT_LAG):
-                    project(*divmod(i, PAIR))
+                    project(*pair_and_half(i))
                 for i in tile_of(step, SCORES_LAG):
                     scores(i)
                 for i in tile_of(step, TURN_LAG):
-                    copy_e(i)
+                    copy_e(i, BOTH, nc.scalar.copy)
                 for i in tile_of(step, ATTEND_LAG):
                     divide(i)
                 for i in tile_of(step, QUANTISE_LAG):
-                    quantise_e(i)
+                    quantise_e(i, BOTH)
                 for i in tile_of(step, FINISH_LAG):
-                    finish(*divmod(i, PAIR))
-                for matrix, g, half in weight_steps[step] if 0 <= step < len(weight_steps) else []:
+                    finish(*pair_and_half(i))
+                for matrix, g, half in weight_steps.get(step, []):
                     turn_weights(matrix, g, half)
                     group_weights(matrix, g, half)
-                for pair in pair_of(step, TURN_ATT_LAG):
-                    group_att([PAIR * pair, PAIR * pair + 1], "scalar" if pair % 3 == 1 and pair < 13 else "vector")
-                for pair in pair_of(step, QUANTISE_ATT_LAG):
-                    quantise_att(pair)
-                for pair in pair_of(step, SUM_LAG):
-                    join_sums(pair)
+                for tiles in pair_of(step, TURN_ATT_LAG):
+                    group_att(tiles, vector_copy)
+                for tiles in pair_of(step, QUANTISE_ATT_LAG):
+                    quantise_att(tiles)
+            turn_e(30, BOTH)
+            turn_att([26, 27])
+            exponentials(31)
+            attend(28)
+            project([24, 25], [0, 1])
+            copy_e(30, BOTH, scalar_copy)
+            quantise_e(29, BOTH)
+            group_att([26, 27], scalar_copy)
+            finish([22, 23], [2, 3])
             join_sums(15)
-            attend(29)
-            turn_e(31)
-            copy_e(31)
-            divide(29)
-            project(12,1)
-            finish(12,0)
-            quantise_e(30)
-            quantise_att(13)
-            finish(12,1)
             invert_sums(15)
-            quantise_e(31)
+            turn_e(31, [0])
+            copy_e(31, [0], vector_copy)
+            attend(29)
+            turn_e(31, [1])
+            copy_e(31, [1], scalar_copy)
+            project([24, 25], [2, 3])
+            divide(28)
+            divide(29)
+            quantise_e(30, BOTH)
+            quantise_e(31, [0])
+            quantise_att([26, 27])
+            quantise_e(31, [1])
             attend(30)
-            divide(30)
-            turn_att([28,29])
-            group_att([28,29],"vector")
-            project(13,0)
             attend(31)
+            divide(30)
             divide(31)
-            quantise_att(14)
-            finish(13,0)
+            finish([24, 25], [0, 1])
+            finish([24, 25], [2, 3])
+            project([26, 27], [0, 1])
+            project([26, 27], [2, 3])
+            turn_att([28, 29])
+            finish([26, 27], [0, 1])
+            group_att([28, 29], vector_copy)
             turn_att([30])
-            group_att([30],"scalar")
-            project(13,1)
-            project(14,0)
-            finish(13,1)
+            group_att([30], scalar_copy)
+            quantise_att([28, 29])
             turn_att([31])
-            group_att([31],"scalar")
-            project(14,1)
-            finish(14,0)
-            quantise_att(15)
-            finish(14,1)
-            project(15,0)
-            project(15,1)
-            finish(15,0)
-            finish(15,1)
+            group_att([31], scalar_copy)
+            finish([26, 27], [2, 3])
+            quantise_att([30])
+            project([28, 29], [0, 1])
+            project([28, 29], [2, 3])
+            project([30], [0, 1, 2, 3])
+            finish([28, 29], [0, 1])
+            quantise_att([31])
+            project([31], [0, 1, 2, 3])
+            finish([28, 29], [2, 3])
+            finish([30], [0, 1, 2, 3])
+            finish([31], [0, 1, 2, 3])

@@ -34,7 +34,7 @@ SCORES_LAG = -2
 TURN_LAG = 1
 QUANTISE_LAG = 2
 SUM_LAG = 1
-INVERT_LAG = 1
+INVERT_LAG = 2
 ATTEND_LAG = 3
 TURN_ATT_LAG = 4
 QUANTISE_ATT_LAG = 5
@@ -81,9 +81,6 @@ def tile_selfattentionconv2d_pb_t_kernel(tc, q, k_pool, v_pool, imgs, w_out, gai
 
         ident_f32 = keep.tile([P, P], F32)
         make_identity(nc, ident_f32[:])
-
-        minus_one = keep.tile([P, PAIR], F32)
-        nc.gpsimd.memset(minus_one[:], -1.0)
 
         weights_sb = {"v": v_sb, "w": w_sb}
         weights_passes = {"v": M_PASSES, "w": 1}
@@ -221,7 +218,7 @@ def tile_selfattentionconv2d_pb_t_kernel(tc, q, k_pool, v_pool, imgs, w_out, gai
 
         def invert_sums(pair):
             inverse = by_pair.tile([P, PAIR], F32)
-            nc.gpsimd.tensor_tensor(out=inverse[:], in0=sums_joined[pair][:], in1=minus_one[:], op=ALU.pow)
+            nc.vector.reciprocal(out=inverse[:], in_=sums_joined[pair][:])
             inverse_sums[pair] = inverse
 
         def attend(i):
@@ -326,10 +323,6 @@ def tile_selfattentionconv2d_pb_t_kernel(tc, q, k_pool, v_pool, imgs, w_out, gai
 
         with tc.manual_schedule():
             for step in range(SCORES_LAG, TILES - 1):
-                for tiles in pair_of(step, SUM_LAG):
-                    join_sums(tiles[0] // PAIR)
-                for tiles in pair_of(step, INVERT_LAG):
-                    invert_sums(tiles[0] // PAIR)
                 for i in tile_of(step, TURN_LAG):
                     turn_e(i, BOTH)
                 for tiles in pair_of(step, TURN_ATT_LAG):
@@ -338,11 +331,17 @@ def tile_selfattentionconv2d_pb_t_kernel(tc, q, k_pool, v_pool, imgs, w_out, gai
                     exponentials(i)
                 for i in tile_of(step, MAXIMUM_LAG):
                     row_maximum(i)
+                for tiles in pair_of(step, SUM_LAG):
+                    join_sums(tiles[0] // PAIR)
                 if step == 2:
                     quantise_weights("v", 0)
                     quantise_weights("v", 1)
                 if step == 4:
                     quantise_weights("w", 0)
+                for tiles in pair_of(step, INVERT_LAG):
+                    invert_sums(tiles[0] // PAIR)
+                for i in tile_of(step, FINISH_LAG):
+                    finish(*pair_and_half(i))
                 for i in tile_of(step, ATTEND_LAG):
                     attend(i)
                 for i in tile_of(step, PROJECT_LAG):
@@ -355,18 +354,17 @@ def tile_selfattentionconv2d_pb_t_kernel(tc, q, k_pool, v_pool, imgs, w_out, gai
                     divide(i)
                 for i in tile_of(step, QUANTISE_LAG):
                     quantise_e(i, BOTH)
-                for i in tile_of(step, FINISH_LAG):
-                    finish(*pair_and_half(i))
                 for matrix, g, half in weight_steps.get(step, []):
                     turn_weights(matrix, g, half)
                     group_weights(matrix, g, half)
                 for tiles in pair_of(step, TURN_ATT_LAG):
-                    group_att(tiles, vector_copy)
+                    group_att(tiles, scalar_copy if tiles[0] % 8 == 2 and tiles[0] < 26 else vector_copy)
                 for tiles in pair_of(step, QUANTISE_ATT_LAG):
                     quantise_att(tiles)
             turn_e(30, BOTH)
             turn_att([26, 27])
             exponentials(31)
+            invert_sums(14)
             attend(28)
             project([24, 25], [0, 1])
             copy_e(30, BOTH, scalar_copy)
@@ -374,7 +372,6 @@ def tile_selfattentionconv2d_pb_t_kernel(tc, q, k_pool, v_pool, imgs, w_out, gai
             group_att([26, 27], scalar_copy)
             finish([22, 23], [2, 3])
             join_sums(15)
-            invert_sums(15)
             turn_e(31, [0])
             copy_e(31, [0], vector_copy)
             attend(29)
@@ -387,6 +384,7 @@ def tile_selfattentionconv2d_pb_t_kernel(tc, q, k_pool, v_pool, imgs, w_out, gai
             quantise_e(31, [0])
             quantise_att([26, 27])
             quantise_e(31, [1])
+            invert_sums(15)
             attend(30)
             attend(31)
             divide(30)

@@ -49,7 +49,7 @@ def tile_selfattentionconv2d_pb_t_kernel(tc, q, k_pool, v_pool, imgs, w_out, gai
     with ExitStack() as ctx:
         keep = ctx.enter_context(tc.tile_pool(name="keep", bufs=1))
         small = ctx.enter_context(tc.tile_pool(name="small", bufs=4))
-        work = ctx.enter_context(tc.tile_pool(name="work", bufs=QUANTISE_LAG + 1))
+        work = ctx.enter_context(tc.tile_pool(name="work", bufs=5))
         codes = ctx.enter_context(tc.tile_pool(name="codes", bufs=ATTEND_LAG - QUANTISE_LAG + 2))
         by_pair = ctx.enter_context(tc.tile_pool(name="by_pair", bufs=4))
         stores = ctx.enter_context(tc.tile_pool(name="stores", bufs=8))
@@ -358,57 +358,57 @@ def tile_selfattentionconv2d_pb_t_kernel(tc, q, k_pool, v_pool, imgs, w_out, gai
                     turn_weights(matrix, g, half)
                     group_weights(matrix, g, half)
                 for tiles in pair_of(step, TURN_ATT_LAG):
-                    group_att(tiles, scalar_copy if tiles[0] % 8 == 2 and tiles[0] < 26 else vector_copy)
+                    group_att(tiles, vector_copy)
                 for tiles in pair_of(step, QUANTISE_ATT_LAG):
                     quantise_att(tiles)
             turn_e(30, BOTH)
             turn_att([26, 27])
             exponentials(31)
-            invert_sums(14)
             attend(28)
             project([24, 25], [0, 1])
             copy_e(30, BOTH, scalar_copy)
             quantise_e(29, BOTH)
-            group_att([26, 27], scalar_copy)
             finish([22, 23], [2, 3])
             join_sums(15)
+            invert_sums(14)
+            group_att([26, 27], vector_copy)
             turn_e(31, [0])
             copy_e(31, [0], vector_copy)
-            attend(29)
             turn_e(31, [1])
+            attend(29)
+            divide(28)
             copy_e(31, [1], scalar_copy)
             project([24, 25], [2, 3])
-            divide(28)
-            divide(29)
             quantise_e(30, BOTH)
             quantise_e(31, [0])
             quantise_att([26, 27])
             quantise_e(31, [1])
-            invert_sums(15)
+            divide(29)
             attend(30)
             attend(31)
+            invert_sums(15)
+            finish([24, 25], [0, 1])
             divide(30)
             divide(31)
-            finish([24, 25], [0, 1])
+            turn_att([28, 29])
             finish([24, 25], [2, 3])
             project([26, 27], [0, 1])
             project([26, 27], [2, 3])
-            turn_att([28, 29])
-            finish([26, 27], [0, 1])
-            group_att([28, 29], vector_copy)
+            group_att([28, 29], scalar_copy)
             turn_att([30])
             group_att([30], scalar_copy)
+            finish([26, 27], [0, 1])
             quantise_att([28, 29])
             turn_att([31])
             group_att([31], scalar_copy)
-            finish([26, 27], [2, 3])
             quantise_att([30])
             project([28, 29], [0, 1])
             project([28, 29], [2, 3])
             project([30], [0, 1, 2, 3])
-            finish([28, 29], [0, 1])
+            finish([26, 27], [2, 3])
             quantise_att([31])
             project([31], [0, 1, 2, 3])
+            finish([28, 29], [0, 1])
             finish([28, 29], [2, 3])
             finish([30], [0, 1, 2, 3])
             finish([31], [0, 1, 2, 3])

@@ -123,6 +123,7 @@ def tile_selfattentionconv2d_pb_t_kernel(tc, q, k_pool, v_pool, imgs, w_out, gai
             )
 
         s_banks = {}
+        bank_maxima = {}
         minus_maxima = {}
         e_rows = {}
         e_turned = {}
@@ -138,26 +139,29 @@ def tile_selfattentionconv2d_pb_t_kernel(tc, q, k_pool, v_pool, imgs, w_out, gai
         att_packed = {}
         y_banks = {}
 
-        def scores(i):
-            s_banks[i] = [psum.tile([P, K_PASS], F32, name="s_ps", tag="bank") for g in range(M_PASSES)]
-            for g in range(M_PASSES):
-                nc.tensor.matmul(
-                    out=s_banks[i][g][:],
-                    lhsT=q_sb[:, i * P : (i + 1) * P],
-                    rhs=k_sb[:, g * K_PASS : (g + 1) * K_PASS],
-                    start=True,
-                    stop=True,
-                )
+        def scores(i, g):
+            s_ps = psum.tile([P, K_PASS], F32, tag="bank")
+            nc.tensor.matmul(
+                out=s_ps[:],
+                lhsT=q_sb[:, i * P : (i + 1) * P],
+                rhs=k_sb[:, g * K_PASS : (g + 1) * K_PASS],
+                start=True,
+                stop=True,
+            )
+            s_banks[(i, g)] = s_ps
 
         def row_maximum(i):
             bank_max = small.tile([P, M_PASSES], F32)
             for g in range(M_PASSES):
-                nc.vector.reduce_max(out=bank_max[:, g : g + 1], in_=s_banks[i][g][:], axis=AX.X)
+                nc.vector.reduce_max(out=bank_max[:, g : g + 1], in_=s_banks[(i, g)][:], axis=AX.X)
+            bank_maxima[i] = bank_max
+
+        def join_maxima(i):
             minus_max = small.tile([P, 1], F32)
-            (nc.vector if i == 0 else nc.gpsimd).tensor_scalar(
+            nc.vector.tensor_scalar(
                 out=minus_max[:],
-                in0=bank_max[:, 0:1],
-                scalar1=bank_max[:, 1:2],
+                in0=bank_maxima[i][:, 0:1],
+                scalar1=bank_maxima[i][:, 1:2],
                 scalar2=-1.0,
                 op0=ALU.max,
                 op1=ALU.mult,
@@ -172,7 +176,7 @@ def tile_selfattentionconv2d_pb_t_kernel(tc, q, k_pool, v_pool, imgs, w_out, gai
             for g in range(M_PASSES):
                 nc.scalar.activation(
                     out=e_sb[:, g * K_PASS : (g + 1) * K_PASS],
-                    in_=s_banks[i][g][:],
+                    in_=s_banks[(i, g)][:],
                     func=ACT.Exp,
                     bias=minus_maxima[i][:],
                     scale=1.0,
@@ -213,7 +217,7 @@ def tile_selfattentionconv2d_pb_t_kernel(tc, q, k_pool, v_pool, imgs, w_out, gai
 
         def join_sums(pair):
             sums = small.tile([P, PAIR], F32)
-            nc.gpsimd.tensor_tensor(out=sums[:], in0=row_sums[pair][:, :, 0], in1=row_sums[pair][:, :, 1], op=ALU.add)
+            nc.vector.tensor_tensor(out=sums[:], in0=row_sums[pair][:, :, 0], in1=row_sums[pair][:, :, 1], op=ALU.add)
             sums_joined[pair] = sums
 
         def invert_sums(pair):
@@ -331,15 +335,19 @@ def tile_selfattentionconv2d_pb_t_kernel(tc, q, k_pool, v_pool, imgs, w_out, gai
                     exponentials(i)
                 for i in tile_of(step, MAXIMUM_LAG):
                     row_maximum(i)
-                for tiles in pair_of(step, SUM_LAG):
-                    join_sums(tiles[0] // PAIR)
+                for tiles in pair_of(step, INVERT_LAG):
+                    invert_sums(tiles[0] // PAIR)
+                for i in tile_of(step, QUANTISE_LAG):
+                    quantise_e(i, BOTH)
                 if step == 2:
                     quantise_weights("v", 0)
                     quantise_weights("v", 1)
                 if step == 4:
                     quantise_weights("w", 0)
-                for tiles in pair_of(step, INVERT_LAG):
-                    invert_sums(tiles[0] // PAIR)
+                for i in tile_of(step, MAXIMUM_LAG):
+                    join_maxima(i)
+                for tiles in pair_of(step, SUM_LAG):
+                    join_sums(tiles[0] // PAIR)
                 for i in tile_of(step, FINISH_LAG):
                     finish(*pair_and_half(i))
                 for i in tile_of(step, ATTEND_LAG):
@@ -347,18 +355,17 @@ def tile_selfattentionconv2d_pb_t_kernel(tc, q, k_pool, v_pool, imgs, w_out, gai
                 for i in tile_of(step, PROJECT_LAG):
                     project(*pair_and_half(i))
                 for i in tile_of(step, SCORES_LAG):
-                    scores(i)
+                    scores(i, 0)
+                    scores(i, 1)
                 for i in tile_of(step, TURN_LAG):
                     copy_e(i, BOTH, nc.scalar.copy)
                 for i in tile_of(step, ATTEND_LAG):
                     divide(i)
-                for i in tile_of(step, QUANTISE_LAG):
-                    quantise_e(i, BOTH)
                 for matrix, g, half in weight_steps.get(step, []):
                     turn_weights(matrix, g, half)
                     group_weights(matrix, g, half)
                 for tiles in pair_of(step, TURN_ATT_LAG):
-                    group_att(tiles, vector_copy)
+                    group_att(tiles, scalar_copy if tiles[0] % 6 == 2 and tiles[0] < 26 else vector_copy)
                 for tiles in pair_of(step, QUANTISE_ATT_LAG):
                     quantise_att(tiles)
             turn_e(30, BOTH)

@@ -309,7 +309,7 @@ def tile_selfattentionconv2d_pb_t_kernel(tc, q, k_pool, v_pool, imgs, w_out, gai
             )
             nc.sync.dma_start(out=out_view[:, span, cols], in_=result[:])
 
-        weight_steps = {0: [("v", 0, 0), ("v", 1, 0)], 1: [("v", 0, 1), ("v", 1, 1)], 2: [("w", 0, 0)], 3: [("w", 0, 1)]}
+        weight_steps = {0: [("v", 0, 0), ("v", 1, 0)], 1: [("v", 0, 1), ("v", 1, 1)], 3: [("w", 0, 0)], 4: [("w", 0, 1)]}
 
         BOTH = [0, 1]
         vector_copy = nc.vector.tensor_copy
@@ -333,23 +333,24 @@ def tile_selfattentionconv2d_pb_t_kernel(tc, q, k_pool, v_pool, imgs, w_out, gai
                     turn_att(tiles)
                 for i in tile_of(step, 0):
                     exponentials(i)
-                for i in tile_of(step, MAXIMUM_LAG):
-                    row_maximum(i)
                 for tiles in pair_of(step, INVERT_LAG):
                     invert_sums(tiles[0] // PAIR)
+                for i in tile_of(step, MAXIMUM_LAG):
+                    row_maximum(i)
                 for i in tile_of(step, QUANTISE_LAG):
                     quantise_e(i, BOTH)
-                if step == 2:
-                    quantise_weights("v", 0)
-                    quantise_weights("v", 1)
-                if step == 4:
-                    quantise_weights("w", 0)
                 for i in tile_of(step, MAXIMUM_LAG):
                     join_maxima(i)
-                for tiles in pair_of(step, SUM_LAG):
-                    join_sums(tiles[0] // PAIR)
                 for i in tile_of(step, FINISH_LAG):
                     finish(*pair_and_half(i))
+                for tiles in pair_of(step, SUM_LAG):
+                    join_sums(tiles[0] // PAIR)
+                if step == 2:
+                    quantise_weights("v", 0)
+                if step == 2:
+                    quantise_weights("v", 1)
+                if step == 5:
+                    quantise_weights("w", 0)
                 for i in tile_of(step, ATTEND_LAG):
                     attend(i)
                 for i in tile_of(step, PROJECT_LAG):

from contextlib import ExitStack

import concourse.mybir as mybir
from concourse.masks import make_identity

F32 = mybir.dt.float32
BF16 = mybir.dt.bfloat16
U32 = mybir.dt.uint32
U8 = mybir.dt.uint8
FP8X4 = mybir.dt.float8_e4m3fn_x4
ACT = mybir.ActivationFunctionType
ALU = mybir.AluOpType
AX = mybir.AxisListType

P = 128
PACK = 4
PAIR = 2
K_PASS = P * PACK
PSUM_BANKS = 8
N_PIX = 4096
M_POS = 1024
DV = 512
C_OUT = 512
M_PASSES = M_POS // K_PASS
TILES = N_PIX // P
GROUP = K_PASS // P
GROUPS = TILES // GROUP
CHUNKS = DV // P
assert DV == K_PASS and C_OUT == DV and CHUNKS == GROUP == PACK
assert M_PASSES == 2

MAXIMUM_LAG = -1
SCORES_LAG = -2
TURN_LAG = 1
QUANTISE_LAG = 2
SUM_LAG = 1
INVERT_LAG = 2
ATTEND_LAG = 3
TURN_ATT_LAG = 4
QUANTISE_ATT_LAG = 5
PROJECT_LAG = QUANTISE_ATT_LAG + PAIR
FINISH_LAG = PROJECT_LAG + 1

FLOPS = 2 * N_PIX * M_POS * P + 2 * N_PIX * M_POS * DV + 2 * N_PIX * DV * C_OUT


def tile_selfattentionconv2d_pb_t_kernel(tc, q, k_pool, v_pool, imgs, w_out, gain, out):
    nc = tc.nc
    with ExitStack() as ctx:
        keep = ctx.enter_context(tc.tile_pool(name="keep", bufs=1))
        small = ctx.enter_context(tc.tile_pool(name="small", bufs=4))
        work = ctx.enter_context(tc.tile_pool(name="work", bufs=5))
        codes = ctx.enter_context(tc.tile_pool(name="codes", bufs=ATTEND_LAG - QUANTISE_LAG + 2))
        by_pair = ctx.enter_context(tc.tile_pool(name="by_pair", bufs=4))
        stores = ctx.enter_context(tc.tile_pool(name="stores", bufs=8))
        psum = ctx.enter_context(tc.psum_pool(name="psum", bufs=PSUM_BANKS))

        q_sb = keep.tile([P, N_PIX], BF16)
        k_sb = keep.tile([P, M_POS], BF16)
        v_sb = keep.tile([P, CHUNKS, M_POS], BF16)
        w_sb = keep.tile([P, CHUNKS, DV], BF16)
        imgs_sb = keep.tile([P, CHUNKS, N_PIX], BF16)
        gain_bf = keep.tile([P, 1], BF16)
        q_view = q.rearrange("b d n -> (b d) n")
        k_view = k_pool.rearrange("b d m -> (b d) m")
        imgs_view = imgs.rearrange("b (c p) h w -> p (b c) (h w)", p=P)
        out_view = out.rearrange("b (c p) h w -> p (b c) (h w)", p=P)
        first = GROUP * P
        nc.sync.dma_start(out=q_sb[:, 0:first], in_=q_view[:, 0:first])
        for g in range(M_PASSES):
            nc.sync.dma_start(out=k_sb[:, g * K_PASS : (g + 1) * K_PASS], in_=k_view[:, g * K_PASS : (g + 1) * K_PASS])
        v_view = v_pool.rearrange("b (c p) m -> p (b c) m", p=P)
        for u in range(PAIR):
            nc.sync.dma_start(out=v_sb[:, PAIR * u : PAIR * (u + 1), :], in_=v_view[:, PAIR * u : PAIR * (u + 1), :])
        nc.sync.dma_start(out=q_sb[:, first : N_PIX // 2], in_=q_view[:, first : N_PIX // 2])
        nc.sync.dma_start(out=w_sb[:], in_=w_out.rearrange("(c p) d -> p c d", p=P))
        nc.sync.dma_start(out=q_sb[:, N_PIX // 2 : N_PIX], in_=q_view[:, N_PIX // 2 : N_PIX])
        for c in range(CHUNKS):
            nc.sync.dma_start(out=imgs_sb[:, c, :], in_=imgs_view[:, c, :])
        nc.sync.dma_start(out=gain_bf[:], in_=gain.partition_broadcast(P))

        ident_f32 = keep.tile([P, P], F32)
        make_identity(nc, ident_f32[:])

        weights_sb = {"v": v_sb, "w": w_sb}
        weights_passes = {"v": M_PASSES, "w": 1}
        weights_grouped = {}
        weights_words = {}
        weights_scales = {}
        for matrix in ("v", "w"):
            shape = [P, weights_passes[matrix], CHUNKS * P]
            weights_grouped[matrix] = keep.tile(shape + [PACK], BF16, align_bytes=64, name=matrix + "_grouped")
            weights_words[matrix] = keep.tile(shape, U32, align_bytes=64, name=matrix + "_words")
            weights_scales[matrix] = keep.tile(shape, U8, align_bytes=64, name=matrix + "_scales")
        weights_turned = {}

        def turn_weights(matrix, g, half):
            turned = psum.tile([P, PAIR * PAIR, P], F32, tag="bank", name="turned")
            for r in range(PAIR):
                row_words = weights_sb[matrix][:, PAIR * half + r, :].bitcast(F32)
                for u in range(PAIR):
                    first_word = (PAIR * g + u) * P
                    nc.tensor.transpose(
                        turned[:, PAIR * r + u, :], row_words[:, first_word : first_word + P], ident_f32[:]
                    )
            weights_turned[(matrix, g, half)] = turned

        def group_weights(matrix, g, half):
            rows = slice(PAIR * half * P, PAIR * (half + 1) * P)
            grouped_words = weights_grouped[matrix][:, g, rows, :].rearrange("p n t -> p (n t)").bitcast(F32)
            out_words = grouped_words.rearrange("p (r n u) -> p r n u", r=PAIR, u=PAIR)
            in_words = weights_turned[(matrix, g, half)][:].rearrange("p (r u) n -> p r n u", u=PAIR)
            if g == 0:
                nc.vector.tensor_copy(out=out_words, in_=in_words)
            else:
                nc.scalar.copy(out=out_words, in_=in_words)

        def quantise_weights(matrix, g):
            nc.vector.quantize_mx(
                out=weights_words[matrix][:, g, :].bitcast(FP8X4),
                scales=weights_scales[matrix][:, g, :],
                in_=weights_grouped[matrix][:, g, :, :].rearrange("p n t -> p (n t)"),
            )

        s_banks = {}
        bank_maxima = {}
        minus_maxima = {}
        e_rows = {}
        e_turned = {}
        e_grouped = {}
        e_packed = {}
        row_sums = {}
        sums_joined = {}
        inverse_sums = {}
        att_banks = {}
        att_rows = {}
        att_turned = {}
        att_grouped = {}
        att_packed = {}
        y_banks = {}

        def scores(i, g):
            s_ps = psum.tile([P, K_PASS], F32, tag="bank")
            nc.tensor.matmul(
                out=s_ps[:],
                lhsT=q_sb[:, i * P : (i + 1) * P],
                rhs=k_sb[:, g * K_PASS : (g + 1) * K_PASS],
                start=True,
                stop=True,
            )
            s_banks[(i, g)] = s_ps

        def row_maximum(i):
            bank_max = small.tile([P, M_PASSES], F32)
            for g in range(M_PASSES):
                nc.vector.reduce_max(out=bank_max[:, g : g + 1], in_=s_banks[(i, g)][:], axis=AX.X)
            bank_maxima[i] = bank_max

        def join_maxima(i):
            minus_max = small.tile([P, 1], F32)
            nc.vector.tensor_scalar(
                out=minus_max[:],
                in0=bank_maxima[i][:, 0:1],
                scalar1=bank_maxima[i][:, 1:2],
                scalar2=-1.0,
                op0=ALU.max,
                op1=ALU.mult,
            )
            minus_maxima[i] = minus_max

        def exponentials(i):
            pair, j = divmod(i, PAIR)
            if j == 0:
                row_sums[pair] = by_pair.tile([P, PAIR, M_PASSES], F32, name="row_sums")
            e_sb = work.tile([P, M_POS], BF16)
            for g in range(M_PASSES):
                nc.scalar.activation(
                    out=e_sb[:, g * K_PASS : (g + 1) * K_PASS],
                    in_=s_banks[(i, g)][:],
                    func=ACT.Exp,
                    bias=minus_maxima[i][:],
                    scale=1.0,
                    accum_out=row_sums[pair][:, j, g : g + 1],
                )
            e_rows[i] = e_sb

        def turn_e(i, passes):
            turned = psum.tile([P, PAIR * len(passes), P], F32, tag="bank", name="e_turned")
            row_words = e_rows[i][:].bitcast(F32)
            for n in range(PAIR * len(passes)):
                block = PAIR * passes[0] + n
                nc.tensor.transpose(turned[:, n, :], row_words[:, block * P : (block + 1) * P], ident_f32[:])
            e_turned[(i, passes[0])] = turned

        def copy_e(i, passes, engine):
            if passes[0] == 0:
                e_grouped[i] = work.tile([P, M_PASSES, P, PACK], BF16, align_bytes=64, name="e_grouped")
            grouped = e_grouped[i][:, passes[0] : passes[-1] + 1, :, :].rearrange("p g n t -> p (g n t)").bitcast(F32)
            engine(
                out=grouped.rearrange("p (g n u) -> p g n u", g=len(passes), u=PAIR),
                in_=e_turned[(i, passes[0])][:].rearrange("p (g u) n -> p g n u", u=PAIR),
            )

        def quantise_e(i, passes):
            if passes[0] == 0:
                e_packed[i] = (
                    codes.tile([P, M_PASSES, P], U32, align_bytes=64, name="e_words"),
                    codes.tile([P, M_PASSES, P], U8, align_bytes=64, name="e_scales"),
                )
            words, scales = e_packed[i]
            span = slice(passes[0], passes[-1] + 1)
            nc.vector.quantize_mx(
                out=words[:, span, :].rearrange("p g n -> p (g n)").bitcast(FP8X4),
                scales=scales[:, span, :].rearrange("p g n -> p (g n)"),
                in_=e_grouped[i][:, span, :, :].rearrange("p g n t -> p (g n t)"),
            )

        def join_sums(pair):
            sums = small.tile([P, PAIR], F32)
            nc.vector.tensor_tensor(out=sums[:], in0=row_sums[pair][:, :, 0], in1=row_sums[pair][:, :, 1], op=ALU.add)
            sums_joined[pair] = sums

        def invert_sums(pair):
            inverse = by_pair.tile([P, PAIR], F32)
            nc.vector.reciprocal(out=inverse[:], in_=sums_joined[pair][:])
            inverse_sums[pair] = inverse

        def attend(i):
            words, scales = e_packed[i]
            att_ps = psum.tile([P, DV], F32, tag="bank", name="att_ps")
            for g in range(M_PASSES):
                nc.tensor.matmul_mx(
                    out=att_ps[:],
                    lhsT=words[:, g, :].bitcast(FP8X4),
                    lhsT_scale=scales[:, g, :],
                    rhs=weights_words["v"][:, g, :].bitcast(FP8X4),
                    rhs_scale=weights_scales["v"][:, g, :],
                    start=(g == 0),
                    stop=(g == M_PASSES - 1),
                )
            att_banks[i] = att_ps

        def divide(i):
            pair, j = divmod(i, PAIR)
            att = work.tile([P, DV], BF16, name="att_rows")
            nc.scalar.activation(out=att[:], in_=att_banks[i][:], func=ACT.Copy, scale=inverse_sums[pair][:, j : j + 1])
            att_rows[i] = att

        def turn_att(tiles):
            turned = psum.tile([P, PAIR * len(tiles), P], F32, tag="bank", name="att_turned")
            for j, i in enumerate(tiles):
                row_words = att_rows[i][:].bitcast(F32)
                for u in range(PAIR):
                    nc.tensor.transpose(turned[:, PAIR * j + u, :], row_words[:, u * P : (u + 1) * P], ident_f32[:])
            att_turned[tiles[0]] = turned

        def group_att(tiles, engine):
            pair, j = divmod(tiles[0], PAIR)
            if j == 0:
                att_grouped[pair] = by_pair.tile([P, PAIR, P, PACK], BF16, align_bytes=64, name="att_grouped")
            grouped = att_grouped[pair][:, j : j + len(tiles), :, :].rearrange("p j n t -> p (j n t)").bitcast(F32)
            out_words = grouped.rearrange("p (j n u) -> p j n u", j=len(tiles), u=PAIR)
            in_words = att_turned[tiles[0]][:].rearrange("p (j u) n -> p j n u", u=PAIR)
            engine(out=out_words, in_=in_words)

        def quantise_att(tiles):
            pair, j = divmod(tiles[0], PAIR)
            if j == 0:
                att_packed[pair] = (
                    by_pair.tile([P, PAIR, P], U32, align_bytes=64, name="att_words"),
                    by_pair.tile([P, PAIR, P], U8, align_bytes=64, name="att_scales"),
                )
            words, scales = att_packed[pair]
            span = slice(j, j + len(tiles))
            nc.vector.quantize_mx(
                out=words[:, span, :].rearrange("p j n -> p (j n)").bitcast(FP8X4),
                scales=scales[:, span, :].rearrange("p j n -> p (j n)"),
                in_=att_grouped[pair][:, span, :, :].rearrange("p j n t -> p (j n t)"),
            )

        def project(tiles, chunks):
            pair, j = divmod(tiles[0], PAIR)
            words, scales = att_packed[pair]
            span = slice(j, j + len(tiles))
            y_ps = psum.tile([P, len(chunks), len(tiles) * P], F32, tag="bank", name="y_ps")
            for n, c in enumerate(chunks):
                nc.tensor.matmul_mx(
                    out=y_ps[:, n, :],
                    lhsT=weights_words["w"][:, 0, c * P : (c + 1) * P].bitcast(FP8X4),
                    lhsT_scale=weights_scales["w"][:, 0, c * P : (c + 1) * P],
                    rhs=words[:, span, :].rearrange("p j n -> p (j n)").bitcast(FP8X4),
                    rhs_scale=scales[:, span, :].rearrange("p j n -> p (j n)"),
                    start=True,
                    stop=True,
                )
            y_banks[(tiles[0], chunks[0])] = y_ps

        def finish(tiles, chunks):
            span = slice(chunks[0], chunks[-1] + 1)
            cols = slice(tiles[0] * P, (tiles[-1] + 1) * P)
            result = stores.tile([P, len(chunks), len(tiles) * P], F32)
            nc.vector.scalar_tensor_tensor(
                out=result[:],
                in0=y_banks[(tiles[0], chunks[0])][:],
                scalar=gain_bf[:, 0:1],
                in1=imgs_sb[:, span, cols],
                op0=ALU.mult,
                op1=ALU.add,
            )
            nc.sync.dma_start(out=out_view[:, span, cols], in_=result[:])

        weight_steps = {0: [("v", 0, 0), ("v", 1, 0)], 1: [("v", 0, 1), ("v", 1, 1)], 3: [("w", 0, 0)], 4: [("w", 0, 1)]}

        BOTH = [0, 1]
        vector_copy = nc.vector.tensor_copy
        scalar_copy = nc.scalar.copy

        def tile_of(step, lag):
            return [step - lag] if 0 <= step - lag < TILES else []

        def pair_of(step, lag):
            return [[i - 1, i] for i in tile_of(step, lag) if i % PAIR == PAIR - 1]

        def pair_and_half(i):
            pair, half = divmod(i, PAIR)
            return [PAIR * pair, PAIR * pair + 1], [PAIR * half, PAIR * half + 1]

        with tc.manual_schedule():
            for step in range(SCORES_LAG, TILES - 1):
                for i in tile_of(step, TURN_LAG):
                    turn_e(i, BOTH)
                for tiles in pair_of(step, TURN_ATT_LAG):
                    turn_att(tiles)
                for i in tile_of(step, 0):
                    exponentials(i)
                for tiles in pair_of(step, INVERT_LAG):
                    invert_sums(tiles[0] // PAIR)
                for i in tile_of(step, MAXIMUM_LAG):
                    row_maximum(i)
                for i in tile_of(step, QUANTISE_LAG):
                    quantise_e(i, BOTH)
                for i in tile_of(step, MAXIMUM_LAG):
                    join_maxima(i)
                for i in tile_of(step, FINISH_LAG):
                    finish(*pair_and_half(i))
                for tiles in pair_of(step, SUM_LAG):
                    join_sums(tiles[0] // PAIR)
                if step == 2:
                    quantise_weights("v", 0)
                if step == 2:
                    quantise_weights("v", 1)
                if step == 5:
                    quantise_weights("w", 0)
                for i in tile_of(step, ATTEND_LAG):
                    attend(i)
                for i in tile_of(step, PROJECT_LAG):
                    project(*pair_and_half(i))
                for i in tile_of(step, SCORES_LAG):
                    scores(i, 0)
                    scores(i, 1)
                for i in tile_of(step, TURN_LAG):
                    copy_e(i, BOTH, nc.scalar.copy)
                for i in tile_of(step, ATTEND_LAG):
                    divide(i)
                for matrix, g, half in weight_steps.get(step, []):
                    turn_weights(matrix, g, half)
                    group_weights(matrix, g, half)
                for tiles in pair_of(step, TURN_ATT_LAG):
                    group_att(tiles, scalar_copy if tiles[0] % 6 == 2 and tiles[0] < 26 else vector_copy)
                for tiles in pair_of(step, QUANTISE_ATT_LAG):
                    quantise_att(tiles)
            turn_e(30, BOTH)
            turn_att([26, 27])
            exponentials(31)
            attend(28)
            project([24, 25], [0, 1])
            copy_e(30, BOTH, scalar_copy)
            quantise_e(29, BOTH)
            finish([22, 23], [2, 3])
            join_sums(15)
            invert_sums(14)
            group_att([26, 27], vector_copy)
            turn_e(31, [0])
            copy_e(31, [0], vector_copy)
            turn_e(31, [1])
            attend(29)
            divide(28)
            copy_e(31, [1], scalar_copy)
            project([24, 25], [2, 3])
            quantise_e(30, BOTH)
            quantise_e(31, [0])
            quantise_att([26, 27])
            quantise_e(31, [1])
            divide(29)
            attend(30)
            attend(31)
            invert_sums(15)
            finish([24, 25], [0, 1])
            divide(30)
            divide(31)
            turn_att([28, 29])
            finish([24, 25], [2, 3])
            project([26, 27], [0, 1])
            project([26, 27], [2, 3])
            group_att([28, 29], scalar_copy)
            turn_att([30])
            group_att([30], scalar_copy)
            finish([26, 27], [0, 1])
            quantise_att([28, 29])
            turn_att([31])
            group_att([31], scalar_copy)
            quantise_att([30])
            project([28, 29], [0, 1])
            project([28, 29], [2, 3])
            project([30], [0, 1, 2, 3])
            finish([26, 27], [2, 3])
            quantise_att([31])
            project([31], [0, 1, 2, 3])
            finish([28, 29], [0, 1])
            finish([28, 29], [2, 3])
            finish([30], [0, 1, 2, 3])
            finish([31], [0, 1, 2, 3])
